import numpy as np
import ml_dtypes


def mxq(x, axis, fmt="e4m3"):
    dtype, down = {"e4m3": (ml_dtypes.float8_e4m3fn, 7), "e5m2": (ml_dtypes.float8_e5m2, 14)}[fmt]
    v = np.moveaxis(np.asarray(x, np.float32).astype(ml_dtypes.bfloat16).astype(np.float64), axis, -1)
    blocks = v.reshape(v.shape[:-1] + (-1, 32))
    amax = np.abs(blocks).max(-1, keepdims=True)
    byte = np.maximum(np.where(amax > 0, np.frexp(amax)[1] - 1 + 127, 0) - down, 1)
    scale = np.exp2(byte - 127.0)
    codes = (blocks / scale).astype(np.float32).astype(dtype).astype(np.float64)
    return np.moveaxis((codes * scale).reshape(v.shape), -1, axis)


WIDE = False


def mx_kscale(k):
    if not WIDE:
        return np.ones(k)
    levels = np.array([10, -10, 5, -5, 0])
    a = np.random.permutation(np.resize(levels, k // 512 * 4)).reshape(k // 512, 4)
    idx = np.arange(k)
    return np.exp2(a[idx // 512, idx % 128 // 32])


BF16 = ml_dtypes.bfloat16


def bf(x):
    return np.asarray(x, np.float32).astype(BF16)


def f64(x):
    return np.asarray(x).astype(np.float64)


B, C, W, H, O = 4096, 64, 4, 4, 1024
K = C * W * H
G = np.sqrt(W * H)
SLO, SHI = 1.0 + 0.03 * G, 2.0 + 0.25 * G


def setup_inputs():
    t = mx_kscale(K).reshape(C, W * H)[np.arange(C), np.arange(C) * (W * H) // C].reshape(1, C, 1, 1)
    return {"x": bf(np.random.standard_normal((B, C, W, H)) * t),
            "cx": bf(np.random.uniform(-W / 2.0, W / 2.0, (O, 1, 1, 1))),
            "cy": bf(np.random.uniform(-H / 2.0, H / 2.0, (O, 1, 1, 1))),
            "sigma": bf(np.random.uniform(SLO, SHI, (O, 1, 1, 1))),
            "features": bf(np.random.standard_normal((O, C, 1, 1)) * 2.0 / (np.sqrt(C) * (SLO + SHI)) / t),
            "bias": bf(np.random.standard_normal(O))}


def reference(x, cx, cy, sigma, features, bias):
    x, cx, cy, sigma, features, bias = f64(x), f64(cx), f64(cy), f64(sigma), f64(features), f64(bias)
    w_edge = (W - 1) / 2.0
    h_edge = (H - 1) / 2.0
    grid_x = np.linspace(-w_edge, w_edge, W).reshape(1, 1, W, 1)
    grid_y = np.linspace(-h_edge, h_edge, H).reshape(1, 1, 1, H)
    d = (cx - grid_x) ** 2 + (cy - grid_y) ** 2
    spatial = np.exp(-d / sigma ** 2)
    weight = (spatial * features).reshape(O, K)
    return (mxq(x.reshape(B, K), 1, "e4m3") @ mxq(weight, 1, "e4m3").T) + bias

@@ -1,0 +1,329 @@
+from contextlib import ExitStack
+
+import concourse.bass as bass
+import concourse.mybir as mybir
+import concourse.tile as tile
+from concourse.masks import make_identity
+
+F32 = mybir.dt.float32
+BF16 = mybir.dt.bfloat16
+U32 = mybir.dt.uint32
+U8 = mybir.dt.uint8
+FP8X4 = mybir.dt.float8_e4m3fn_x4
+ALU = mybir.AluOpType
+ACT = mybir.ActivationFunctionType
+
+P = 128
+B, C, O, K = 4096, 64, 1024, 1024
+FLOPS = 2 * B * K * O
+
+PIN = True
+GUNITS = ()
+EO_STEADY = "VVSVSVSV"
+EO_LAST = "VVVVVVVV"
+LOOKAHEAD = 2
+TPB = 3
+HEAD_WHO = "SSSS" + "SSSS" + "VVVV" + "VSVS"
+UNIT_ORDER = ((0, 0), (1, 0), (0, 1), (1, 1), (0, 2), (1, 2), (0, 3), (1, 3))
+
+
+def tile_gaussianspatialxfeaturelinear_t_kernel(tc, x, cx, cy, sigma, features, bias, out):
+    nc = tc.nc
+    with ExitStack() as ctx:
+        const = ctx.enter_context(tc.tile_pool(name="const", bufs=1))
+        xin = ctx.enter_context(tc.tile_pool(name="xin", bufs=1))
+        stage = ctx.enter_context(tc.tile_pool(name="stage", bufs=3))
+        outp = ctx.enter_context(tc.tile_pool(name="outp", bufs=6))
+        psum = ctx.enter_context(tc.psum_pool(name="psum", bufs=4))
+        if PIN:
+            ctx.enter_context(tc.manual_schedule())
+
+        xv = x.rearrange("(n j p r) c w h -> n p j (r c w h)", j=2, p=P, r=2)
+        xlast = x.rearrange("(j r p) c w h -> j p r (c w h)", r=2, p=P)
+        ov = out.rearrange("(j p r) o -> j p r o", p=P, r=2)
+        olast = out.rearrange("(j r p) o -> j p r o", r=2, p=P)
+        fv = features.rearrange("(t p) c x y -> p t (c x y)", p=P)
+
+        ident_b = const.tile([P, P], BF16, name="ident_b")
+        ident_f = const.tile([P, P], F32, name="ident_f")
+        make_identity(nc, ident_b[:])
+        make_identity(nc, ident_f[:])
+        zrows = const.tile([P, P], BF16, name="zrows")
+        nc.vector.memset(zrows[:], 0.0)
+        brow = const.tile([P, O], BF16, name="brow")
+        nc.vector.memset(brow[:], 0.0)
+        ones_b = const.tile([P, P], BF16, name="ones_b")
+        nc.vector.memset(ones_b[:], 1.0)
+        warm = const.tile([P, 1], F32, name="warm")
+        nc.vector.memset(warm[:], 0.0)
+        grid = const.tile([P, 4], F32, name="grid")
+        for i in range(4):
+            nc.vector.memset(grid[:, i : i + 1], i - 1.5)
+        sel = const.tile([P, 8 * P], BF16, name="sel")
+        nc.vector.tensor_copy(
+            out=sel[:].rearrange("p (r k) -> p r k", k=8),
+            in_=ident_b[:].unsqueeze(2).to_broadcast([P, P, 8]),
+        )
+
+        for j, v in enumerate((cx, cy, sigma)):
+            nc.sync.dma_start(out=zrows[8 * j : 8 * j + 8, :], in_=v.rearrange("(t p) a b c -> t (p a b c)", p=P))
+        nc.scalar.dma_start(out=brow[0:1, :], in_=bias.rearrange("(a o) -> a o", a=1))
+        fsb = const.tile([P, 8, C], BF16, name="fsb")
+        nc.sync.dma_start(out=fsb[:], in_=fv)
+        xs = []
+        for ch in range(8):
+            xt = xin.tile([P, 4, K], BF16, name="x%d" % ch)
+            xs.append(xt)
+            xt2 = xt[:].rearrange("p (j r) k -> p j (r k)", j=2)
+            if ch == 0:
+                nc.sync.dma_start(out=xt2[:, 0:1, :], in_=xv[ch][:, 0:1, :])
+                nc.sync.dma_start(out=xt2[:, 1:2, :], in_=xv[ch][:, 1:2, :])
+            elif ch == 7:
+                nc.sync.dma_start(out=xt2[:, 0:1, :], in_=xv[ch][:, 0:1, :])
+                nc.sync.dma_start(out=xt[:, 2:4, :], in_=xlast[15])
+            else:
+                nc.sync.dma_start(out=xt2, in_=xv[ch])
+        warm2 = const.tile([P, 1], F32, name="warm2")
+        nc.scalar.activation(out=warm2[:], in_=warm[:], func=ACT.Exp)
+
+        gw = const.tile([P, 2, O, 4], BF16, name="gw", align_bytes=64)
+        wcod = const.tile([P, 2, O], U32, name="wcod", align_bytes=64)
+        wscl = const.tile([P, 2, O], U8, name="wscl", align_bytes=64)
+        xcod = [const.tile([P, 1024], U32, name="xcod%d" % ch, align_bytes=64) for ch in range(8)]
+        xscl = [const.tile([P, 1024], U8, name="xscl%d" % ch, align_bytes=64) for ch in range(8)]
+        bias_sb = const.tile([P, O], BF16, name="bias_sb")
+        stsb = const.tile([P, 4, 2, 256], F32, name="stsb")
+        ftsb = const.tile([P, 4 * P], BF16, name="ftsb")
+        gxs = {}
+
+        def stage_a(ch, engines="SSSS"):
+            gx = stage.tile([P, 4, K], BF16, name="gx", align_bytes=64)
+            gxs[ch] = gx
+            tps = []
+            for r in range(4):
+                tp = psum.tile([P, 4, P], F32, name="tp", tag="tp", bufs=TPB)
+                xw = xs[ch][:, r, :].bitcast(F32)
+                for s in range(4):
+                    nc.tensor.transpose(tp[:, s, :], xw[:, P * s : P * s + P], ident_f[:])
+                tps.append(tp)
+            for r in range(4):
+                dst = gx[:, r, :].bitcast(F32).rearrange("p (g b u) -> p g b u", g=2, u=2)
+                src = tps[r][:].rearrange("p (g u) b -> p g b u", g=2)
+                if engines[r] == "S":
+                    nc.scalar.copy(out=dst, in_=src)
+                else:
+                    nc.vector.tensor_copy(out=dst, in_=src)
+
+        def quant_x(ch):
+            nc.vector.quantize_mx(
+                out=xcod[ch][:].bitcast(FP8X4),
+                scales=xscl[ch][:],
+                in_=gxs[ch][:].rearrange("p r k -> p (r k)"),
+            )
+
+        def mm(ch, r, h):
+            acc = psum.tile([P, 512], F32, name="acc", tag="acc", bufs=8 - TPB)
+            for g in range(2):
+                c0 = r * 256 + g * P
+                nc.tensor.matmul_mx(
+                    out=acc[:],
+                    lhsT=xcod[ch][:, c0 : c0 + P].bitcast(FP8X4),
+                    lhsT_scale=xscl[ch][:, c0 : c0 + P],
+                    rhs=wcod[:, g, 512 * h : 512 * h + 512].bitcast(FP8X4),
+                    rhs_scale=wscl[:, g, 512 * h : 512 * h + 512],
+                    start=(g == 0),
+                    stop=(g == 1),
+                )
+            return acc
+
+        def empty(acc, dst, h, who):
+            bsl = bias_sb[:, 512 * h : 512 * h + 512]
+            if who == "V":
+                nc.vector.tensor_tensor(out=dst, in0=acc[:], in1=bsl, op=ALU.add)
+            else:
+                nc.scalar.copy(out=dst, in_=acc[:])
+                nc.gpsimd.tensor_tensor(out=dst, in0=dst, in1=bsl, op=ALU.add)
+
+        pz = psum.tile([P, P], BF16, name="pz", tag="tp", bufs=TPB)
+        nc.tensor.transpose(pz[:], zrows[:], ident_b[:])
+        zt = const.tile([P, 24], F32, name="zt")
+        nc.vector.tensor_copy(out=zt[:], in_=pz[:, 0:24])
+        pf = psum.tile([P, 4, P], BF16, name="pf", tag="tp", bufs=TPB)
+        for a in range(4):
+            nc.tensor.transpose(pf[:, a, :], fsb[:, 2 * a : 2 * a + 2, :].rearrange("p t c -> p (t c)"), ident_b[:])
+
+        dxy = const.tile([P, 2, 8, 4], F32, name="dxy")
+        nc.vector.tensor_tensor(
+            out=dxy[:],
+            in0=zt[:, 0:16].rearrange("p (a t) -> p a t", a=2).unsqueeze(3).to_broadcast([P, 2, 8, 4]),
+            in1=grid[:].unsqueeze(1).unsqueeze(1).to_broadcast([P, 2, 8, 4]),
+            op=ALU.subtract,
+        )
+        sq = const.tile([P, 2, 8, 4], F32, name="sq")
+        nc.vector.tensor_tensor(out=sq[:], in0=dxy[:], in1=dxy[:], op=ALU.mult)
+        s2 = const.tile([P, 8], F32, name="s2")
+        nc.vector.tensor_tensor(out=s2[:], in0=zt[:, 16:24], in1=zt[:, 16:24], op=ALU.mult)
+        rinv = const.tile([P, 8], F32, name="rinv")
+        nc.vector.reciprocal(out=rinv[:], in_=s2[:])
+        dd = const.tile([P, 8, 2, 4, 2], F32, name="dd")
+        for e in range(2):
+            nc.vector.tensor_tensor(
+                out=dd[:, :, e, :, :],
+                in0=sq[:, 0, :, :].unsqueeze(3).to_broadcast([P, 8, 4, 2]),
+                in1=sq[:, 1, :, e::2].unsqueeze(2).to_broadcast([P, 8, 4, 2]),
+                op=ALU.add,
+            )
+        qq = const.tile([P, 8, 16], F32, name="qq")
+        nc.vector.tensor_tensor(
+            out=qq[:],
+            in0=dd[:].rearrange("p t e i j -> p t (e i j)"),
+            in1=rinv[:].unsqueeze(2).to_broadcast([P, 8, 16]),
+            op=ALU.mult,
+        )
+        nc.vector.tensor_copy(out=ftsb[:], in_=pf[:].rearrange("p a o -> p (a o)"))
+
+        def exp_q(q):
+            sx = stage.tile([P, 4, P], F32, name="sx", bufs=2)
+            nc.scalar.activation(
+                out=sx[:].rearrange("p s (c j) -> p s c j", j=8),
+                in_=qq[:, 2 * q : 2 * q + 2, :].rearrange("p t (e j) -> p (t e) j", e=2).unsqueeze(2).to_broadcast([P, 4, 16, 8]),
+                func=ACT.Exp,
+                scale=-1.0,
+            )
+            return sx
+
+        def st_t(q, sx):
+            pst = psum.tile([P, 4, P], F32, name="pst", tag="tp", bufs=TPB)
+            for e in range(2):
+                for tl in range(2):
+                    nc.tensor.transpose(pst[:, 2 * e + tl, :], sx[:, 2 * tl + e, :], ident_f[:])
+            return pst
+
+        def st_ev(q, pst):
+            nc.scalar.copy(out=stsb[:, q, :, :], in_=pst[:].rearrange("p (e t) o -> p e (t o)", e=2))
+
+        def ft_unit(g, q):
+            pft = psum.tile([P, 2, 256], F32, name="pft", tag="acc", bufs=8 - TPB)
+            for u in range(2):
+                for tl in range(2):
+                    m = 4 * tl + 2 * g + u
+                    nc.tensor.matmul(
+                        out=pft[:, u, P * tl : P * tl + P],
+                        lhsT=sel[:, P * m : P * m + P],
+                        rhs=ftsb[:, P * q : P * q + P],
+                        start=True,
+                        stop=True,
+                    )
+            return pft
+
+        def product(g, q, pft):
+            dst = gw[:, g, 256 * q : 256 * q + 256, :].rearrange("p o (u e) -> p o u e", u=2)
+            st = stsb[:, q, :, :].rearrange("p e o -> p o e").unsqueeze(2).to_broadcast([P, 256, 2, 2])
+            if (g, q) in GUNITS:
+                ftx = stage.tile([P, 2, 256], BF16, name="ftx", bufs=2)
+                nc.scalar.copy(out=ftx[:], in_=pft[:])
+                for half in range(2):
+                    sl = slice(128 * half, 128 * half + 128)
+                    nc.gpsimd.tensor_tensor(
+                        out=dst[:, sl],
+                        in0=ftx[:].rearrange("p u o -> p o u").unsqueeze(3).to_broadcast([P, 256, 2, 2])[:, sl],
+                        in1=st[:, sl],
+                        op=ALU.mult,
+                    )
+            else:
+                nc.vector.tensor_tensor(
+                    out=dst,
+                    in0=pft[:].rearrange("p u o -> p o u").unsqueeze(3).to_broadcast([P, 256, 2, 2]),
+                    in1=st,
+                    op=ALU.mult,
+                )
+
+        def quant_w(g, h):
+            nc.vector.quantize_mx(
+                out=wcod[:, g, 512 * h : 512 * h + 512].bitcast(FP8X4),
+                scales=wscl[:, g, 512 * h : 512 * h + 512],
+                in_=gw[:, g, 512 * h : 512 * h + 512, :].rearrange("p o t -> p (o t)"),
+            )
+
+        osbs = {}
+
+        def group(ch, r, h, who):
+            if (ch, r // 2) not in osbs:
+                osbs[(ch, r // 2)] = outp.tile([P, 2, O], F32, name="osb")
+            acc = mm(ch, r, h)
+            empty(acc, osbs[(ch, r // 2)][:, r % 2, 512 * h : 512 * h + 512], h, who)
+
+        def store(ch, r0, n):
+            j = 2 * ch + r0 // 2
+            if n == 2:
+                nc.sync.dma_start(out=ov[j], in_=osbs[(ch, r0 // 2)][:])
+            else:
+                nc.sync.dma_start(out=olast[j][:, r0 % 2 : r0 % 2 + 1, :], in_=osbs[(ch, r0 // 2)][:, r0 % 2 : r0 % 2 + 1, :])
+
+        sx0 = exp_q(0)
+        sx1 = exp_q(1)
+        pfts = {}
+        pst0 = st_t(0, sx0)
+        st_ev(0, pst0)
+        pfts[(0, 0)] = ft_unit(0, 0)
+        pfts[(1, 0)] = ft_unit(1, 0)
+        pst1 = st_t(1, sx1)
+        sx2 = exp_q(2)
+        st_ev(1, pst1)
+        sx3 = exp_q(3)
+        pfts[(0, 1)] = ft_unit(0, 1)
+        pfts[(1, 1)] = ft_unit(1, 1)
+        pst2 = st_t(2, sx2)
+        st_ev(2, pst2)
+        pst3 = st_t(3, sx3)
+        st_ev(3, pst3)
+        pb = psum.tile([P, O], BF16, name="pb", tag="tp", bufs=TPB)
+        for h in range(2):
+            nc.tensor.matmul(out=pb[:, 512 * h : 512 * h + 512], lhsT=ones_b[:], rhs=brow[:, 512 * h : 512 * h + 512], start=True, stop=True)
+        nc.scalar.copy(out=bias_sb[:], in_=pb[:])
+        stage_a(0)
+        for g, q in ((0, 0), (1, 0), (0, 1), (1, 1)):
+            product(g, q, pfts[(g, q)])
+        pfts[(0, 2)] = ft_unit(0, 2)
+        pfts[(1, 2)] = ft_unit(1, 2)
+        stage_a(1)
+        quant_w(0, 0)
+        quant_w(1, 0)
+        quant_x(0)
+        for r in range(4):
+            group(0, r, 0, HEAD_WHO[r])
+        product(0, 2, pfts[(0, 2)])
+        product(1, 2, pfts[(1, 2)])
+        pfts[(0, 3)] = ft_unit(0, 3)
+        pfts[(1, 3)] = ft_unit(1, 3)
+        stage_a(2)
+        quant_x(1)
+        for r in range(4):
+            group(1, r, 0, HEAD_WHO[4 + r])
+        product(0, 3, pfts[(0, 3)])
+        product(1, 3, pfts[(1, 3)])
+        quant_w(0, 1)
+        quant_w(1, 1)
+        if LOOKAHEAD > 1:
+            stage_a(3)
+        for ch in range(2):
+            for r in range(4):
+                group(ch, r, 1, HEAD_WHO[8 + 4 * ch + r])
+                if r % 2 == 1:
+                    store(ch, r - 1, 2)
+            if ch == 0:
+                quant_x(2)
+
+        for ch in range(2, 8):
+            if ch + LOOKAHEAD < 8 and ch + LOOKAHEAD not in gxs:
+                stage_a(ch + LOOKAHEAD)
+            who = EO_LAST if ch == 7 else EO_STEADY
+            for r in range(4):
+                for h in range(2):
+                    group(ch, r, h, who[2 * r + h])
+                if ch == 7 and r >= 2:
+                    store(ch, r, 1)
+                elif r % 2 == 1:
+                    store(ch, r - 1, 2)
+                if r == 0 and ch + 1 < 8:
+                    quant_x(ch + 1)

@@ -17,7 +17,7 @@ P = 128
 B, C, O, K = 4096, 64, 1024, 1024
 FLOPS = 2 * B * K * O
 
-PIN = True
+PIN = False
 GUNITS = ()
 EO_STEADY = "VVSVSVSV"
 EO_LAST = "VVVVVVVV"

@@ -17,10 +17,17 @@ P = 128
 B, C, O, K = 4096, 64, 1024, 1024
 FLOPS = 2 * B * K * O
 
-PIN = False
+PIN = True
 GUNITS = ()
-EO_STEADY = "VVSVSVSV"
-EO_LAST = "VVVVVVVV"
+EO_STEADY = "VSVVVSVV"
+EO_LAST = "SVVVVVVV"
+EO_6 = "SVVVSVVV"
+QX0_SPLIT = True
+HALF = False
+QPOS = 5
+TILE_CH = (7,)
+QX1_FIRST = False
+S_EARLY_X = True
 LOOKAHEAD = 2
 TPB = 3
 HEAD_WHO = "SSSS" + "SSSS" + "VVVV" + "VSVS"
@@ -39,9 +46,9 @@ def tile_gaussianspatialxfeaturelinear_t_kernel(tc, x, cx, cy, sigma, features, 
             ctx.enter_context(tc.manual_schedule())
 
         xv = x.rearrange("(n j p r) c w h -> n p j (r c w h)", j=2, p=P, r=2)
-        xlast = x.rearrange("(j r p) c w h -> j p r (c w h)", r=2, p=P)
+        xtile = x.rearrange("(n r p) c w h -> n p r (c w h)", r=4, p=P)
         ov = out.rearrange("(j p r) o -> j p r o", p=P, r=2)
-        olast = out.rearrange("(j r p) o -> j p r o", r=2, p=P)
+        otile = out.rearrange("(n r p) o -> n p r o", r=4, p=P)
         fv = features.rearrange("(t p) c x y -> p t (c x y)", p=P)
 
         ident_b = const.tile([P, P], BF16, name="ident_b")
@@ -69,7 +76,6 @@ def tile_gaussianspatialxfeaturelinear_t_kernel(tc, x, cx, cy, sigma, features, 
             nc.sync.dma_start(out=zrows[8 * j : 8 * j + 8, :], in_=v.rearrange("(t p) a b c -> t (p a b c)", p=P))
         nc.scalar.dma_start(out=brow[0:1, :], in_=bias.rearrange("(a o) -> a o", a=1))
         fsb = const.tile([P, 8, C], BF16, name="fsb")
-        nc.sync.dma_start(out=fsb[:], in_=fv)
         xs = []
         for ch in range(8):
             xt = xin.tile([P, 4, K], BF16, name="x%d" % ch)
@@ -77,10 +83,10 @@ def tile_gaussianspatialxfeaturelinear_t_kernel(tc, x, cx, cy, sigma, features, 
             xt2 = xt[:].rearrange("p (j r) k -> p j (r k)", j=2)
             if ch == 0:
                 nc.sync.dma_start(out=xt2[:, 0:1, :], in_=xv[ch][:, 0:1, :])
+                nc.sync.dma_start(out=fsb[:], in_=fv)
                 nc.sync.dma_start(out=xt2[:, 1:2, :], in_=xv[ch][:, 1:2, :])
-            elif ch == 7:
-                nc.sync.dma_start(out=xt2[:, 0:1, :], in_=xv[ch][:, 0:1, :])
-                nc.sync.dma_start(out=xt[:, 2:4, :], in_=xlast[15])
+            elif ch in TILE_CH:
+                nc.sync.dma_start(out=xt[:], in_=xtile[ch])
             else:
                 nc.sync.dma_start(out=xt2, in_=xv[ch])
         warm2 = const.tile([P, 1], F32, name="warm2")
@@ -96,29 +102,36 @@ def tile_gaussianspatialxfeaturelinear_t_kernel(tc, x, cx, cy, sigma, features, 
         ftsb = const.tile([P, 4 * P], BF16, name="ftsb")
         gxs = {}
 
-        def stage_a(ch, engines="SSSS"):
-            gx = stage.tile([P, 4, K], BF16, name="gx", align_bytes=64)
-            gxs[ch] = gx
-            tps = []
-            for r in range(4):
-                tp = psum.tile([P, 4, P], F32, name="tp", tag="tp", bufs=TPB)
-                xw = xs[ch][:, r, :].bitcast(F32)
-                for s in range(4):
-                    nc.tensor.transpose(tp[:, s, :], xw[:, P * s : P * s + P], ident_f[:])
-                tps.append(tp)
-            for r in range(4):
-                dst = gx[:, r, :].bitcast(F32).rearrange("p (g b u) -> p g b u", g=2, u=2)
-                src = tps[r][:].rearrange("p (g u) b -> p g b u", g=2)
-                if engines[r] == "S":
-                    nc.scalar.copy(out=dst, in_=src)
-                else:
-                    nc.vector.tensor_copy(out=dst, in_=src)
+        tps = {}
 
-        def quant_x(ch):
+        def tx(ch, r):
+            tp = psum.tile([P, 4, P], F32, name="tp", tag="tp", bufs=TPB)
+            xw = xs[ch][:, r, :].bitcast(F32)
+            for s in range(4):
+                nc.tensor.transpose(tp[:, s, :], xw[:, P * s : P * s + P], ident_f[:])
+            tps[(ch, r)] = tp
+
+        def ex(ch, r, who="S"):
+            if ch not in gxs:
+                gxs[ch] = stage.tile([P, 4, K], BF16, name="gx", align_bytes=64)
+            dst = gxs[ch][:, r, :].bitcast(F32).rearrange("p (g b u) -> p g b u", g=2, u=2)
+            src = tps[(ch, r)][:].rearrange("p (g u) b -> p g b u", g=2)
+            if who == "S":
+                nc.scalar.copy(out=dst, in_=src)
+            else:
+                nc.vector.tensor_copy(out=dst, in_=src)
+
+        def stage_a(ch):
+            for r in range(4):
+                tx(ch, r)
+            for r in range(4):
+                ex(ch, r)
+
+        def quant_x(ch, lo=0, n=4):
             nc.vector.quantize_mx(
-                out=xcod[ch][:].bitcast(FP8X4),
-                scales=xscl[ch][:],
-                in_=gxs[ch][:].rearrange("p r k -> p (r k)"),
+                out=xcod[ch][:, 256 * lo : 256 * (lo + n)].bitcast(FP8X4),
+                scales=xscl[ch][:, 256 * lo : 256 * (lo + n)],
+                in_=gxs[ch][:, lo : lo + n, :].rearrange("p r k -> p (r k)"),
             )
 
         def mm(ch, r, h):
@@ -144,13 +157,10 @@ def tile_gaussianspatialxfeaturelinear_t_kernel(tc, x, cx, cy, sigma, features, 
                 nc.scalar.copy(out=dst, in_=acc[:])
                 nc.gpsimd.tensor_tensor(out=dst, in0=dst, in1=bsl, op=ALU.add)
 
-        pz = psum.tile([P, P], BF16, name="pz", tag="tp", bufs=TPB)
+        pz = psum.tile([P, P], BF16, name="pz", tag="acc", bufs=8 - TPB)
         nc.tensor.transpose(pz[:], zrows[:], ident_b[:])
         zt = const.tile([P, 24], F32, name="zt")
         nc.vector.tensor_copy(out=zt[:], in_=pz[:, 0:24])
-        pf = psum.tile([P, 4, P], BF16, name="pf", tag="tp", bufs=TPB)
-        for a in range(4):
-            nc.tensor.transpose(pf[:, a, :], fsb[:, 2 * a : 2 * a + 2, :].rearrange("p t c -> p (t c)"), ident_b[:])
 
         dxy = const.tile([P, 2, 8, 4], F32, name="dxy")
         nc.vector.tensor_tensor(
@@ -180,7 +190,6 @@ def tile_gaussianspatialxfeaturelinear_t_kernel(tc, x, cx, cy, sigma, features, 
             in1=rinv[:].unsqueeze(2).to_broadcast([P, 8, 16]),
             op=ALU.mult,
         )
-        nc.vector.tensor_copy(out=ftsb[:], in_=pf[:].rearrange("p a o -> p (a o)"))
 
         def exp_q(q):
             sx = stage.tile([P, 4, P], F32, name="sx", bufs=2)
@@ -253,26 +262,48 @@ def tile_gaussianspatialxfeaturelinear_t_kernel(tc, x, cx, cy, sigma, features, 
             acc = mm(ch, r, h)
             empty(acc, osbs[(ch, r // 2)][:, r % 2, 512 * h : 512 * h + 512], h, who)
 
+        def store_half(ch, pair, h):
+            j = 2 * ch + pair
+            nc.sync.dma_start(out=ov[j][:, :, 512 * h : 512 * h + 512], in_=osbs[(ch, pair)][:, :, 512 * h : 512 * h + 512])
+
         def store(ch, r0, n):
             j = 2 * ch + r0 // 2
             if n == 2:
                 nc.sync.dma_start(out=ov[j], in_=osbs[(ch, r0 // 2)][:])
             else:
-                nc.sync.dma_start(out=olast[j][:, r0 % 2 : r0 % 2 + 1, :], in_=osbs[(ch, r0 // 2)][:, r0 % 2 : r0 % 2 + 1, :])
+                nc.sync.dma_start(out=otile[ch][:, r0 : r0 + 1, :], in_=osbs[(ch, r0 // 2)][:, r0 % 2 : r0 % 2 + 1, :])
 
+        tx(0, 0)
+        tx(0, 1)
+        pf = psum.tile([P, 4, P], BF16, name="pf", tag="acc", bufs=8 - TPB)
+        for a in range(4):
+            nc.tensor.transpose(pf[:, a, :], fsb[:, 2 * a : 2 * a + 2, :].rearrange("p t c -> p (t c)"), ident_b[:])
         sx0 = exp_q(0)
         sx1 = exp_q(1)
+        ex(0, 0, "V")
+        nc.vector.tensor_copy(out=ftsb[:], in_=pf[:].rearrange("p a o -> p (a o)"))
+        ex(0, 1, "V")
         pfts = {}
         pst0 = st_t(0, sx0)
         st_ev(0, pst0)
         pfts[(0, 0)] = ft_unit(0, 0)
         pfts[(1, 0)] = ft_unit(1, 0)
+        if (1, 0) in GUNITS:
+            product(1, 0, pfts[(1, 0)])
         pst1 = st_t(1, sx1)
         sx2 = exp_q(2)
         st_ev(1, pst1)
         sx3 = exp_q(3)
+        quant_x(0, 0, 2)
         pfts[(0, 1)] = ft_unit(0, 1)
         pfts[(1, 1)] = ft_unit(1, 1)
+        tx(0, 2)
+        tx(0, 3)
+        ex(0, 2)
+        ex(0, 3)
+        for g, q in ((0, 0), (1, 0), (0, 1), (1, 1)):
+            if (g, q) not in GUNITS:
+                product(g, q, pfts[(g, q)])
         pst2 = st_t(2, sx2)
         st_ev(2, pst2)
         pst3 = st_t(3, sx3)
@@ -281,49 +312,61 @@ def tile_gaussianspatialxfeaturelinear_t_kernel(tc, x, cx, cy, sigma, features, 
         for h in range(2):
             nc.tensor.matmul(out=pb[:, 512 * h : 512 * h + 512], lhsT=ones_b[:], rhs=brow[:, 512 * h : 512 * h + 512], start=True, stop=True)
         nc.scalar.copy(out=bias_sb[:], in_=pb[:])
-        stage_a(0)
-        for g, q in ((0, 0), (1, 0), (0, 1), (1, 1)):
-            product(g, q, pfts[(g, q)])
         pfts[(0, 2)] = ft_unit(0, 2)
         pfts[(1, 2)] = ft_unit(1, 2)
         stage_a(1)
         quant_w(0, 0)
         quant_w(1, 0)
-        quant_x(0)
-        for r in range(4):
-            group(0, r, 0, HEAD_WHO[r])
+        group(0, 0, 0, HEAD_WHO[0])
+        group(0, 1, 0, HEAD_WHO[1])
+        if HALF:
+            store_half(0, 0, 0)
+        quant_x(0, 2, 2)
+        group(0, 2, 0, HEAD_WHO[2])
+        group(0, 3, 0, HEAD_WHO[3])
+        if HALF:
+            store_half(0, 1, 0)
+        if QX1_FIRST:
+            quant_x(1)
         product(0, 2, pfts[(0, 2)])
         product(1, 2, pfts[(1, 2)])
         pfts[(0, 3)] = ft_unit(0, 3)
         pfts[(1, 3)] = ft_unit(1, 3)
-        stage_a(2)
-        quant_x(1)
+        if not QX1_FIRST:
+            stage_a(2)
+            quant_x(1)
         for r in range(4):
             group(1, r, 0, HEAD_WHO[4 + r])
+            if HALF and r % 2 == 1:
+                store_half(1, r // 2, 0)
+        if QX1_FIRST:
+            stage_a(2)
         product(0, 3, pfts[(0, 3)])
         product(1, 3, pfts[(1, 3)])
         quant_w(0, 1)
         quant_w(1, 1)
-        if LOOKAHEAD > 1:
-            stage_a(3)
+        stage_a(3)
         for ch in range(2):
             for r in range(4):
                 group(ch, r, 1, HEAD_WHO[8 + 4 * ch + r])
                 if r % 2 == 1:
-                    store(ch, r - 1, 2)
-            if ch == 0:
-                quant_x(2)
+                    if HALF:
+                        store_half(ch, r // 2, 1)
+                    else:
+                        store(ch, r - 1, 2)
+            if ch == 0 or LOOKAHEAD == 2:
+                quant_x(2 + ch)
 
         for ch in range(2, 8):
             if ch + LOOKAHEAD < 8 and ch + LOOKAHEAD not in gxs:
                 stage_a(ch + LOOKAHEAD)
-            who = EO_LAST if ch == 7 else EO_STEADY
+            who = EO_LAST if ch == 7 else (EO_6 if ch == 6 else EO_STEADY)
             for r in range(4):
                 for h in range(2):
+                    if 2 * r + h == QPOS and ch + LOOKAHEAD < 8:
+                        quant_x(ch + LOOKAHEAD)
                     group(ch, r, h, who[2 * r + h])
-                if ch == 7 and r >= 2:
+                if ch in TILE_CH:
                     store(ch, r, 1)
                 elif r % 2 == 1:
                     store(ch, r - 1, 2)
-                if r == 0 and ch + 1 < 8:
-                    quant_x(ch + 1)

@@ -23,7 +23,10 @@ EO_STEADY = "VSVVVSVV"
 EO_LAST = "SVVVVVVV"
 EO_6 = "SVVVSVVV"
 QX0_SPLIT = True
-HALF = False
+EARLY1 = False
+QPOS6 = 3
+STAGE_AT = {2: 4, 3: 5, 4: 6, 5: 7}
+HALF = True
 QPOS = 5
 TILE_CH = (7,)
 QX1_FIRST = False
@@ -45,10 +48,8 @@ def tile_gaussianspatialxfeaturelinear_t_kernel(tc, x, cx, cy, sigma, features, 
         if PIN:
             ctx.enter_context(tc.manual_schedule())
 
-        xv = x.rearrange("(n j p r) c w h -> n p j (r c w h)", j=2, p=P, r=2)
-        xtile = x.rearrange("(n r p) c w h -> n p r (c w h)", r=4, p=P)
-        ov = out.rearrange("(j p r) o -> j p r o", p=P, r=2)
-        otile = out.rearrange("(n r p) o -> n p r o", r=4, p=P)
+        xv = x.rearrange("(n p r) c w h -> n p r (c w h)", p=P, r=4)
+        ov = out.rearrange("(n p r) o -> n p r o", p=P, r=4)
         fv = features.rearrange("(t p) c x y -> p t (c x y)", p=P)
 
         ident_b = const.tile([P, P], BF16, name="ident_b")
@@ -80,15 +81,12 @@ def tile_gaussianspatialxfeaturelinear_t_kernel(tc, x, cx, cy, sigma, features, 
         for ch in range(8):
             xt = xin.tile([P, 4, K], BF16, name="x%d" % ch)
             xs.append(xt)
-            xt2 = xt[:].rearrange("p (j r) k -> p j (r k)", j=2)
             if ch == 0:
-                nc.sync.dma_start(out=xt2[:, 0:1, :], in_=xv[ch][:, 0:1, :])
+                nc.sync.dma_start(out=xt[:, 0:2, :], in_=xv[ch][:, 0:2, :])
                 nc.sync.dma_start(out=fsb[:], in_=fv)
-                nc.sync.dma_start(out=xt2[:, 1:2, :], in_=xv[ch][:, 1:2, :])
-            elif ch in TILE_CH:
-                nc.sync.dma_start(out=xt[:], in_=xtile[ch])
+                nc.sync.dma_start(out=xt[:, 2:4, :], in_=xv[ch][:, 2:4, :])
             else:
-                nc.sync.dma_start(out=xt2, in_=xv[ch])
+                nc.sync.dma_start(out=xt[:], in_=xv[ch])
         warm2 = const.tile([P, 1], F32, name="warm2")
         nc.scalar.activation(out=warm2[:], in_=warm[:], func=ACT.Exp)
 
@@ -212,7 +210,7 @@ def tile_gaussianspatialxfeaturelinear_t_kernel(tc, x, cx, cy, sigma, features, 
             nc.scalar.copy(out=stsb[:, q, :, :], in_=pst[:].rearrange("p (e t) o -> p e (t o)", e=2))
 
         def ft_unit(g, q):
-            pft = psum.tile([P, 2, 256], F32, name="pft", tag="acc", bufs=8 - TPB)
+            pft = psum.tile([P, 2, 256], BF16 if (g, q) in GUNITS else F32, name="pft", tag="acc", bufs=8 - TPB)
             for u in range(2):
                 for tl in range(2):
                     m = 4 * tl + 2 * g + u
@@ -260,18 +258,19 @@ def tile_gaussianspatialxfeaturelinear_t_kernel(tc, x, cx, cy, sigma, features, 
             if (ch, r // 2) not in osbs:
                 osbs[(ch, r // 2)] = outp.tile([P, 2, O], F32, name="osb")
             acc = mm(ch, r, h)
-            empty(acc, osbs[(ch, r // 2)][:, r % 2, 512 * h : 512 * h + 512], h, who)
+            if HALF and ch < 2:
+                empty(acc, osbs[(ch, r // 2)][:, h, 512 * (r % 2) : 512 * (r % 2) + 512], h, who)
+            else:
+                empty(acc, osbs[(ch, r // 2)][:, r % 2, 512 * h : 512 * h + 512], h, who)
 
         def store_half(ch, pair, h):
-            j = 2 * ch + pair
-            nc.sync.dma_start(out=ov[j][:, :, 512 * h : 512 * h + 512], in_=osbs[(ch, pair)][:, :, 512 * h : 512 * h + 512])
+            nc.sync.dma_start(
+                out=ov[ch][:, 2 * pair : 2 * pair + 2, 512 * h : 512 * h + 512],
+                in_=osbs[(ch, pair)][:, h, :].rearrange("p (r o) -> p r o", r=2),
+            )
 
         def store(ch, r0, n):
-            j = 2 * ch + r0 // 2
-            if n == 2:
-                nc.sync.dma_start(out=ov[j], in_=osbs[(ch, r0 // 2)][:])
-            else:
-                nc.sync.dma_start(out=otile[ch][:, r0 : r0 + 1, :], in_=osbs[(ch, r0 // 2)][:, r0 % 2 : r0 % 2 + 1, :])
+            nc.sync.dma_start(out=ov[ch][:, r0 : r0 + n, :], in_=osbs[(ch, r0 // 2)][:, r0 % 2 : r0 % 2 + n, :])
 
         tx(0, 0)
         tx(0, 1)
@@ -301,6 +300,8 @@ def tile_gaussianspatialxfeaturelinear_t_kernel(tc, x, cx, cy, sigma, features, 
         tx(0, 3)
         ex(0, 2)
         ex(0, 3)
+        if EARLY1:
+            stage_a(1)
         for g, q in ((0, 0), (1, 0), (0, 1), (1, 1)):
             if (g, q) not in GUNITS:
                 product(g, q, pfts[(g, q)])
@@ -308,13 +309,18 @@ def tile_gaussianspatialxfeaturelinear_t_kernel(tc, x, cx, cy, sigma, features, 
         st_ev(2, pst2)
         pst3 = st_t(3, sx3)
         st_ev(3, pst3)
+        for u in GUNITS:
+            if u[1] >= 2:
+                product(u[0], u[1], ft_unit(u[0], u[1]))
         pb = psum.tile([P, O], BF16, name="pb", tag="tp", bufs=TPB)
         for h in range(2):
             nc.tensor.matmul(out=pb[:, 512 * h : 512 * h + 512], lhsT=ones_b[:], rhs=brow[:, 512 * h : 512 * h + 512], start=True, stop=True)
         nc.scalar.copy(out=bias_sb[:], in_=pb[:])
-        pfts[(0, 2)] = ft_unit(0, 2)
-        pfts[(1, 2)] = ft_unit(1, 2)
-        stage_a(1)
+        for u in ((0, 2), (1, 2)):
+            if u not in GUNITS:
+                pfts[u] = ft_unit(u[0], u[1])
+        if not EARLY1:
+            stage_a(1)
         quant_w(0, 0)
         quant_w(1, 0)
         group(0, 0, 0, HEAD_WHO[0])
@@ -328,21 +334,22 @@ def tile_gaussianspatialxfeaturelinear_t_kernel(tc, x, cx, cy, sigma, features, 
             store_half(0, 1, 0)
         if QX1_FIRST:
             quant_x(1)
-        product(0, 2, pfts[(0, 2)])
-        product(1, 2, pfts[(1, 2)])
-        pfts[(0, 3)] = ft_unit(0, 3)
-        pfts[(1, 3)] = ft_unit(1, 3)
+        for u in ((0, 2), (1, 2)):
+            if u not in GUNITS:
+                product(u[0], u[1], pfts[u])
+        for u in ((0, 3), (1, 3)):
+            if u not in GUNITS:
+                pfts[u] = ft_unit(u[0], u[1])
         if not QX1_FIRST:
             stage_a(2)
             quant_x(1)
         for r in range(4):
             group(1, r, 0, HEAD_WHO[4 + r])
-            if HALF and r % 2 == 1:
-                store_half(1, r // 2, 0)
         if QX1_FIRST:
             stage_a(2)
-        product(0, 3, pfts[(0, 3)])
-        product(1, 3, pfts[(1, 3)])
+        for u in ((0, 3), (1, 3)):
+            if u not in GUNITS:
+                product(u[0], u[1], pfts[u])
         quant_w(0, 1)
         quant_w(1, 1)
         stage_a(3)
@@ -354,17 +361,21 @@ def tile_gaussianspatialxfeaturelinear_t_kernel(tc, x, cx, cy, sigma, features, 
                         store_half(ch, r // 2, 1)
                     else:
                         store(ch, r - 1, 2)
+            if ch == 0 and HALF:
+                store_half(1, 0, 0)
+                store_half(1, 1, 0)
             if ch == 0 or LOOKAHEAD == 2:
                 quant_x(2 + ch)
 
         for ch in range(2, 8):
-            if ch + LOOKAHEAD < 8 and ch + LOOKAHEAD not in gxs:
-                stage_a(ch + LOOKAHEAD)
+            nxt = STAGE_AT.get(ch)
+            if nxt is not None:
+                stage_a(nxt)
             who = EO_LAST if ch == 7 else (EO_6 if ch == 6 else EO_STEADY)
             for r in range(4):
                 for h in range(2):
-                    if 2 * r + h == QPOS and ch + LOOKAHEAD < 8:
-                        quant_x(ch + LOOKAHEAD)
+                    if 2 * r + h == (QPOS6 if ch == 6 else QPOS) and nxt is not None:
+                        quant_x(nxt)
                     group(ch, r, h, who[2 * r + h])
                 if ch in TILE_CH:
                     store(ch, r, 1)

@@ -1,8 +1,6 @@
 from contextlib import ExitStack
 
-import concourse.bass as bass
 import concourse.mybir as mybir
-import concourse.tile as tile
 from concourse.masks import make_identity
 
 F32 = mybir.dt.float32
@@ -15,26 +13,12 @@ ACT = mybir.ActivationFunctionType
 
 P = 128
 B, C, O, K = 4096, 64, 1024, 1024
+HALF = 512
+QUARTER = 256
+TILES = 4
+CHUNKS = B // (TILES * P)
+TRANSPOSE_BANKS = 3
 FLOPS = 2 * B * K * O
-
-PIN = True
-GUNITS = ()
-EO_STEADY = "VSVVVSVV"
-EO_LAST = "SVVVVVVV"
-EO_6 = "SVVVSVVV"
-QX0_SPLIT = True
-EARLY1 = False
-QPOS6 = 3
-STAGE_AT = {2: 4, 3: 5, 4: 6, 5: 7}
-HALF = True
-QPOS = 5
-TILE_CH = (7,)
-QX1_FIRST = False
-S_EARLY_X = True
-LOOKAHEAD = 2
-TPB = 3
-HEAD_WHO = "SSSS" + "SSSS" + "VVVV" + "VSVS"
-UNIT_ORDER = ((0, 0), (1, 0), (0, 1), (1, 1), (0, 2), (1, 2), (0, 3), (1, 3))
 
 
 def tile_gaussianspatialxfeaturelinear_t_kernel(tc, x, cx, cy, sigma, features, bias, out):
@@ -45,339 +29,293 @@ def tile_gaussianspatialxfeaturelinear_t_kernel(tc, x, cx, cy, sigma, features, 
         stage = ctx.enter_context(tc.tile_pool(name="stage", bufs=3))
         outp = ctx.enter_context(tc.tile_pool(name="outp", bufs=6))
         psum = ctx.enter_context(tc.psum_pool(name="psum", bufs=4))
-        if PIN:
-            ctx.enter_context(tc.manual_schedule())
+        ctx.enter_context(tc.manual_schedule())
 
-        xv = x.rearrange("(n p r) c w h -> n p r (c w h)", p=P, r=4)
-        ov = out.rearrange("(n p r) o -> n p r o", p=P, r=4)
-        fv = features.rearrange("(t p) c x y -> p t (c x y)", p=P)
+        x_chunks = x.rearrange("(n p r) c w h -> n p r (c w h)", p=P, r=TILES)
+        y_chunks = out.rearrange("(n p r) o -> n p r o", p=P, r=TILES)
+
+        def transpose_bank(shape, dtype, name):
+            return psum.tile(shape, dtype, name=name, tag="tp", bufs=TRANSPOSE_BANKS)
+
+        def matmul_bank(shape, dtype, name):
+            return psum.tile(shape, dtype, name=name, tag="acc", bufs=8 - TRANSPOSE_BANKS)
 
         ident_b = const.tile([P, P], BF16, name="ident_b")
         ident_f = const.tile([P, P], F32, name="ident_f")
         make_identity(nc, ident_b[:])
         make_identity(nc, ident_f[:])
-        zrows = const.tile([P, P], BF16, name="zrows")
-        nc.vector.memset(zrows[:], 0.0)
-        brow = const.tile([P, O], BF16, name="brow")
-        nc.vector.memset(brow[:], 0.0)
+        vec_rows = const.tile([P, P], BF16, name="zrows")
+        nc.vector.memset(vec_rows[:], 0.0)
+        bias_row = const.tile([P, O], BF16, name="brow")
+        nc.vector.memset(bias_row[:], 0.0)
         ones_b = const.tile([P, P], BF16, name="ones_b")
         nc.vector.memset(ones_b[:], 1.0)
-        warm = const.tile([P, 1], F32, name="warm")
-        nc.vector.memset(warm[:], 0.0)
+        zero_col = const.tile([P, 1], F32, name="warm")
+        nc.vector.memset(zero_col[:], 0.0)
         grid = const.tile([P, 4], F32, name="grid")
         for i in range(4):
             nc.vector.memset(grid[:, i : i + 1], i - 1.5)
-        sel = const.tile([P, 8 * P], BF16, name="sel")
+        select = const.tile([P, 8 * P], BF16, name="sel")
         nc.vector.tensor_copy(
-            out=sel[:].rearrange("p (r k) -> p r k", k=8),
+            out=select[:].rearrange("p (r s) -> p r s", s=8),
             in_=ident_b[:].unsqueeze(2).to_broadcast([P, P, 8]),
         )
 
-        for j, v in enumerate((cx, cy, sigma)):
-            nc.sync.dma_start(out=zrows[8 * j : 8 * j + 8, :], in_=v.rearrange("(t p) a b c -> t (p a b c)", p=P))
-        nc.scalar.dma_start(out=brow[0:1, :], in_=bias.rearrange("(a o) -> a o", a=1))
-        fsb = const.tile([P, 8, C], BF16, name="fsb")
-        xs = []
-        for ch in range(8):
-            xt = xin.tile([P, 4, K], BF16, name="x%d" % ch)
-            xs.append(xt)
-            if ch == 0:
-                nc.sync.dma_start(out=xt[:, 0:2, :], in_=xv[ch][:, 0:2, :])
-                nc.sync.dma_start(out=fsb[:], in_=fv)
-                nc.sync.dma_start(out=xt[:, 2:4, :], in_=xv[ch][:, 2:4, :])
+        for n, vec in enumerate((cx, cy, sigma)):
+            nc.sync.dma_start(out=vec_rows[8 * n : 8 * n + 8, :], in_=vec.rearrange("(t p) a b c -> t (p a b c)", p=P))
+        nc.scalar.dma_start(out=bias_row[0:1, :], in_=bias.rearrange("(a o) -> a o", a=1))
+        feat = const.tile([P, 8, C], BF16, name="fsb")
+        x_raw = []
+        for n in range(CHUNKS):
+            x_tile = xin.tile([P, TILES, K], BF16, name="x%d" % n)
+            x_raw.append(x_tile)
+            if n == 0:
+                nc.sync.dma_start(out=x_tile[:, 0:2, :], in_=x_chunks[n][:, 0:2, :])
+                nc.sync.dma_start(out=feat[:], in_=features.rearrange("(t p) c a b -> p t (c a b)", p=P))
+                nc.sync.dma_start(out=x_tile[:, 2:4, :], in_=x_chunks[n][:, 2:4, :])
             else:
-                nc.sync.dma_start(out=xt[:], in_=xv[ch])
-        warm2 = const.tile([P, 1], F32, name="warm2")
-        nc.scalar.activation(out=warm2[:], in_=warm[:], func=ACT.Exp)
+                nc.sync.dma_start(out=x_tile[:], in_=x_chunks[n])
+        one_col = const.tile([P, 1], F32, name="warm2")
+        nc.scalar.activation(out=one_col[:], in_=zero_col[:], func=ACT.Exp)
 
-        gw = const.tile([P, 2, O, 4], BF16, name="gw", align_bytes=64)
-        wcod = const.tile([P, 2, O], U32, name="wcod", align_bytes=64)
-        wscl = const.tile([P, 2, O], U8, name="wscl", align_bytes=64)
-        xcod = [const.tile([P, 1024], U32, name="xcod%d" % ch, align_bytes=64) for ch in range(8)]
-        xscl = [const.tile([P, 1024], U8, name="xscl%d" % ch, align_bytes=64) for ch in range(8)]
-        bias_sb = const.tile([P, O], BF16, name="bias_sb")
-        stsb = const.tile([P, 4, 2, 256], F32, name="stsb")
-        ftsb = const.tile([P, 4 * P], BF16, name="ftsb")
-        gxs = {}
+        w_bf16 = const.tile([P, 2, O, 4], BF16, name="gw", align_bytes=64)
+        w_words = const.tile([P, 2, O], U32, name="wcod", align_bytes=64)
+        w_scales = const.tile([P, 2, O], U8, name="wscl", align_bytes=64)
+        x_words = [const.tile([P, TILES * 2 * P], U32, name="xcod%d" % n, align_bytes=64) for n in range(CHUNKS)]
+        x_scales = [const.tile([P, TILES * 2 * P], U8, name="xscl%d" % n, align_bytes=64) for n in range(CHUNKS)]
+        bias_all = const.tile([P, O], BF16, name="bias_sb")
+        spat_t = const.tile([P, 4, 2, QUARTER], F32, name="stsb")
+        feat_t = const.tile([P, 4 * P], BF16, name="ftsb")
+        x_bf16 = {}
+        x_banks = {}
+        y_pairs = {}
 
-        tps = {}
-
-        def tx(ch, r):
-            tp = psum.tile([P, 4, P], F32, name="tp", tag="tp", bufs=TPB)
-            xw = xs[ch][:, r, :].bitcast(F32)
+        def transpose_x(n, r):
+            bank = transpose_bank([P, 4, P], F32, "tp")
+            words = x_raw[n][:, r, :].bitcast(F32)
             for s in range(4):
-                nc.tensor.transpose(tp[:, s, :], xw[:, P * s : P * s + P], ident_f[:])
-            tps[(ch, r)] = tp
+                nc.tensor.transpose(bank[:, s, :], words[:, P * s : P * s + P], ident_f[:])
+            x_banks[(n, r)] = bank
 
-        def ex(ch, r, who="S"):
-            if ch not in gxs:
-                gxs[ch] = stage.tile([P, 4, K], BF16, name="gx", align_bytes=64)
-            dst = gxs[ch][:, r, :].bitcast(F32).rearrange("p (g b u) -> p g b u", g=2, u=2)
-            src = tps[(ch, r)][:].rearrange("p (g u) b -> p g b u", g=2)
-            if who == "S":
+        def regroup_x(n, r, engine):
+            if n not in x_bf16:
+                x_bf16[n] = stage.tile([P, TILES, K], BF16, name="gx", align_bytes=64)
+            dst = x_bf16[n][:, r, :].bitcast(F32).rearrange("p (g b u) -> p g b u", g=2, u=2)
+            src = x_banks[(n, r)][:].rearrange("p (g u) b -> p g b u", g=2)
+            if engine == "scalar":
                 nc.scalar.copy(out=dst, in_=src)
             else:
                 nc.vector.tensor_copy(out=dst, in_=src)
 
-        def stage_a(ch):
-            for r in range(4):
-                tx(ch, r)
-            for r in range(4):
-                ex(ch, r)
+        def stage_chunk(n):
+            for r in range(TILES):
+                transpose_x(n, r)
+            for r in range(TILES):
+                regroup_x(n, r, "scalar")
 
-        def quant_x(ch, lo=0, n=4):
+        def quantise_x(n, first=0, count=TILES):
+            cols = slice(2 * P * first, 2 * P * (first + count))
             nc.vector.quantize_mx(
-                out=xcod[ch][:, 256 * lo : 256 * (lo + n)].bitcast(FP8X4),
-                scales=xscl[ch][:, 256 * lo : 256 * (lo + n)],
-                in_=gxs[ch][:, lo : lo + n, :].rearrange("p r k -> p (r k)"),
+                out=x_words[n][:, cols].bitcast(FP8X4),
+                scales=x_scales[n][:, cols],
+                in_=x_bf16[n][:, first : first + count, :].rearrange("p r k -> p (r k)"),
             )
 
-        def mm(ch, r, h):
-            acc = psum.tile([P, 512], F32, name="acc", tag="acc", bufs=8 - TPB)
+        def multiply(n, r, h, way_out):
+            if (n, r // 2) not in y_pairs:
+                y_pairs[(n, r // 2)] = outp.tile([P, 2, O], F32, name="osb")
+            half = slice(HALF * h, HALF * h + HALF)
+            bank = matmul_bank([P, HALF], F32, "acc")
             for g in range(2):
-                c0 = r * 256 + g * P
+                cols = slice(2 * P * r + P * g, 2 * P * r + P * g + P)
                 nc.tensor.matmul_mx(
-                    out=acc[:],
-                    lhsT=xcod[ch][:, c0 : c0 + P].bitcast(FP8X4),
-                    lhsT_scale=xscl[ch][:, c0 : c0 + P],
-                    rhs=wcod[:, g, 512 * h : 512 * h + 512].bitcast(FP8X4),
-                    rhs_scale=wscl[:, g, 512 * h : 512 * h + 512],
+                    out=bank[:],
+                    lhsT=x_words[n][:, cols].bitcast(FP8X4),
+                    lhsT_scale=x_scales[n][:, cols],
+                    rhs=w_words[:, g, half].bitcast(FP8X4),
+                    rhs_scale=w_scales[:, g, half],
                     start=(g == 0),
                     stop=(g == 1),
                 )
-            return acc
-
-        def empty(acc, dst, h, who):
-            bsl = bias_sb[:, 512 * h : 512 * h + 512]
-            if who == "V":
-                nc.vector.tensor_tensor(out=dst, in0=acc[:], in1=bsl, op=ALU.add)
+            dst = y_pairs[(n, r // 2)][:, r % 2, half]
+            if way_out == "vector":
+                nc.vector.tensor_tensor(out=dst, in0=bank[:], in1=bias_all[:, half], op=ALU.add)
             else:
-                nc.scalar.copy(out=dst, in_=acc[:])
-                nc.gpsimd.tensor_tensor(out=dst, in0=dst, in1=bsl, op=ALU.add)
+                nc.scalar.copy(out=dst, in_=bank[:])
+                nc.gpsimd.tensor_tensor(out=dst, in0=dst, in1=bias_all[:, half], op=ALU.add)
 
-        pz = psum.tile([P, P], BF16, name="pz", tag="acc", bufs=8 - TPB)
-        nc.tensor.transpose(pz[:], zrows[:], ident_b[:])
-        zt = const.tile([P, 24], F32, name="zt")
-        nc.vector.tensor_copy(out=zt[:], in_=pz[:, 0:24])
+        def store(n, first, count):
+            nc.sync.dma_start(
+                out=y_chunks[n][:, first : first + count, :],
+                in_=y_pairs[(n, first // 2)][:, first % 2 : first % 2 + count, :],
+            )
 
-        dxy = const.tile([P, 2, 8, 4], F32, name="dxy")
+        vec_bank = matmul_bank([P, P], BF16, "pz")
+        nc.tensor.transpose(vec_bank[:], vec_rows[:], ident_b[:])
+        vec_cols = const.tile([P, 24], F32, name="zt")
+        nc.vector.tensor_copy(out=vec_cols[:], in_=vec_bank[:, 0:24])
+        dist = const.tile([P, 2, 8, 4], F32, name="dxy")
         nc.vector.tensor_tensor(
-            out=dxy[:],
-            in0=zt[:, 0:16].rearrange("p (a t) -> p a t", a=2).unsqueeze(3).to_broadcast([P, 2, 8, 4]),
+            out=dist[:],
+            in0=vec_cols[:, 0:16].rearrange("p (a t) -> p a t", a=2).unsqueeze(3).to_broadcast([P, 2, 8, 4]),
             in1=grid[:].unsqueeze(1).unsqueeze(1).to_broadcast([P, 2, 8, 4]),
             op=ALU.subtract,
         )
-        sq = const.tile([P, 2, 8, 4], F32, name="sq")
-        nc.vector.tensor_tensor(out=sq[:], in0=dxy[:], in1=dxy[:], op=ALU.mult)
-        s2 = const.tile([P, 8], F32, name="s2")
-        nc.vector.tensor_tensor(out=s2[:], in0=zt[:, 16:24], in1=zt[:, 16:24], op=ALU.mult)
-        rinv = const.tile([P, 8], F32, name="rinv")
-        nc.vector.reciprocal(out=rinv[:], in_=s2[:])
-        dd = const.tile([P, 8, 2, 4, 2], F32, name="dd")
+        dist_sq = const.tile([P, 2, 8, 4], F32, name="sq")
+        nc.vector.tensor_tensor(out=dist_sq[:], in0=dist[:], in1=dist[:], op=ALU.mult)
+        sigma_sq = const.tile([P, 8], F32, name="s2")
+        nc.vector.tensor_tensor(out=sigma_sq[:], in0=vec_cols[:, 16:24], in1=vec_cols[:, 16:24], op=ALU.mult)
+        inv_sigma_sq = const.tile([P, 8], F32, name="rinv")
+        nc.vector.reciprocal(out=inv_sigma_sq[:], in_=sigma_sq[:])
+        dist_sum = const.tile([P, 8, 2, 4, 2], F32, name="dd")
         for e in range(2):
             nc.vector.tensor_tensor(
-                out=dd[:, :, e, :, :],
-                in0=sq[:, 0, :, :].unsqueeze(3).to_broadcast([P, 8, 4, 2]),
-                in1=sq[:, 1, :, e::2].unsqueeze(2).to_broadcast([P, 8, 4, 2]),
+                out=dist_sum[:, :, e, :, :],
+                in0=dist_sq[:, 0, :, :].unsqueeze(3).to_broadcast([P, 8, 4, 2]),
+                in1=dist_sq[:, 1, :, e::2].unsqueeze(2).to_broadcast([P, 8, 4, 2]),
                 op=ALU.add,
             )
-        qq = const.tile([P, 8, 16], F32, name="qq")
+        exponent = const.tile([P, 8, 16], F32, name="qq")
         nc.vector.tensor_tensor(
-            out=qq[:],
-            in0=dd[:].rearrange("p t e i j -> p t (e i j)"),
-            in1=rinv[:].unsqueeze(2).to_broadcast([P, 8, 16]),
+            out=exponent[:],
+            in0=dist_sum[:].rearrange("p t e i j -> p t (e i j)"),
+            in1=inv_sigma_sq[:].unsqueeze(2).to_broadcast([P, 8, 16]),
             op=ALU.mult,
         )
 
-        def exp_q(q):
-            sx = stage.tile([P, 4, P], F32, name="sx", bufs=2)
+        def exp_repeated(q):
+            rep = stage.tile([P, 4, P], F32, name="sx", bufs=2)
             nc.scalar.activation(
-                out=sx[:].rearrange("p s (c j) -> p s c j", j=8),
-                in_=qq[:, 2 * q : 2 * q + 2, :].rearrange("p t (e j) -> p (t e) j", e=2).unsqueeze(2).to_broadcast([P, 4, 16, 8]),
+                out=rep[:].rearrange("p b (s m) -> p b s m", m=8),
+                in_=exponent[:, 2 * q : 2 * q + 2, :]
+                .rearrange("p t (e m) -> p (t e) m", e=2)
+                .unsqueeze(2)
+                .to_broadcast([P, 4, 16, 8]),
                 func=ACT.Exp,
                 scale=-1.0,
             )
-            return sx
+            return rep
 
-        def st_t(q, sx):
-            pst = psum.tile([P, 4, P], F32, name="pst", tag="tp", bufs=TPB)
+        def transpose_spat(rep):
+            bank = transpose_bank([P, 4, P], F32, "pst")
             for e in range(2):
-                for tl in range(2):
-                    nc.tensor.transpose(pst[:, 2 * e + tl, :], sx[:, 2 * tl + e, :], ident_f[:])
-            return pst
+                for t in range(2):
+                    nc.tensor.transpose(bank[:, 2 * e + t, :], rep[:, 2 * t + e, :], ident_f[:])
+            return bank
 
-        def st_ev(q, pst):
-            nc.scalar.copy(out=stsb[:, q, :, :], in_=pst[:].rearrange("p (e t) o -> p e (t o)", e=2))
+        def keep_spat(q, bank):
+            nc.scalar.copy(out=spat_t[:, q, :, :], in_=bank[:].rearrange("p (e t) o -> p e (t o)", e=2))
 
-        def ft_unit(g, q):
-            pft = psum.tile([P, 2, 256], BF16 if (g, q) in GUNITS else F32, name="pft", tag="acc", bufs=8 - TPB)
+        def select_feat(g, q):
+            bank = matmul_bank([P, 2, QUARTER], F32, "pft")
             for u in range(2):
-                for tl in range(2):
-                    m = 4 * tl + 2 * g + u
+                for s in range(2):
+                    m = 4 * s + 2 * g + u
                     nc.tensor.matmul(
-                        out=pft[:, u, P * tl : P * tl + P],
-                        lhsT=sel[:, P * m : P * m + P],
-                        rhs=ftsb[:, P * q : P * q + P],
+                        out=bank[:, u, P * s : P * s + P],
+                        lhsT=select[:, P * m : P * m + P],
+                        rhs=feat_t[:, P * q : P * q + P],
                         start=True,
                         stop=True,
                     )
-            return pft
+            return bank
 
-        def product(g, q, pft):
-            dst = gw[:, g, 256 * q : 256 * q + 256, :].rearrange("p o (u e) -> p o u e", u=2)
-            st = stsb[:, q, :, :].rearrange("p e o -> p o e").unsqueeze(2).to_broadcast([P, 256, 2, 2])
-            if (g, q) in GUNITS:
-                ftx = stage.tile([P, 2, 256], BF16, name="ftx", bufs=2)
-                nc.scalar.copy(out=ftx[:], in_=pft[:])
-                for half in range(2):
-                    sl = slice(128 * half, 128 * half + 128)
-                    nc.gpsimd.tensor_tensor(
-                        out=dst[:, sl],
-                        in0=ftx[:].rearrange("p u o -> p o u").unsqueeze(3).to_broadcast([P, 256, 2, 2])[:, sl],
-                        in1=st[:, sl],
-                        op=ALU.mult,
-                    )
-            else:
-                nc.vector.tensor_tensor(
-                    out=dst,
-                    in0=pft[:].rearrange("p u o -> p o u").unsqueeze(3).to_broadcast([P, 256, 2, 2]),
-                    in1=st,
-                    op=ALU.mult,
-                )
+        def build_w(g, q, feat_bank):
+            shape = [P, QUARTER, 2, 2]
+            nc.vector.tensor_tensor(
+                out=w_bf16[:, g, QUARTER * q : QUARTER * q + QUARTER, :].rearrange("p o (u e) -> p o u e", u=2),
+                in0=feat_bank[:].rearrange("p u o -> p o u").unsqueeze(3).to_broadcast(shape),
+                in1=spat_t[:, q, :, :].rearrange("p e o -> p o e").unsqueeze(2).to_broadcast(shape),
+                op=ALU.mult,
+            )
 
-        def quant_w(g, h):
+        def quantise_w(g, h):
+            half = slice(HALF * h, HALF * h + HALF)
             nc.vector.quantize_mx(
-                out=wcod[:, g, 512 * h : 512 * h + 512].bitcast(FP8X4),
-                scales=wscl[:, g, 512 * h : 512 * h + 512],
-                in_=gw[:, g, 512 * h : 512 * h + 512, :].rearrange("p o t -> p (o t)"),
+                out=w_words[:, g, half].bitcast(FP8X4),
+                scales=w_scales[:, g, half],
+                in_=w_bf16[:, g, half, :].rearrange("p o t -> p (o t)"),
             )
 
-        osbs = {}
-
-        def group(ch, r, h, who):
-            if (ch, r // 2) not in osbs:
-                osbs[(ch, r // 2)] = outp.tile([P, 2, O], F32, name="osb")
-            acc = mm(ch, r, h)
-            if HALF and ch < 2:
-                empty(acc, osbs[(ch, r // 2)][:, h, 512 * (r % 2) : 512 * (r % 2) + 512], h, who)
-            else:
-                empty(acc, osbs[(ch, r // 2)][:, r % 2, 512 * h : 512 * h + 512], h, who)
-
-        def store_half(ch, pair, h):
-            nc.sync.dma_start(
-                out=ov[ch][:, 2 * pair : 2 * pair + 2, 512 * h : 512 * h + 512],
-                in_=osbs[(ch, pair)][:, h, :].rearrange("p (r o) -> p r o", r=2),
-            )
-
-        def store(ch, r0, n):
-            nc.sync.dma_start(out=ov[ch][:, r0 : r0 + n, :], in_=osbs[(ch, r0 // 2)][:, r0 % 2 : r0 % 2 + n, :])
-
-        tx(0, 0)
-        tx(0, 1)
-        pf = psum.tile([P, 4, P], BF16, name="pf", tag="acc", bufs=8 - TPB)
+        transpose_x(0, 0)
+        transpose_x(0, 1)
+        feat_bank_t = matmul_bank([P, 4, P], BF16, "pf")
         for a in range(4):
-            nc.tensor.transpose(pf[:, a, :], fsb[:, 2 * a : 2 * a + 2, :].rearrange("p t c -> p (t c)"), ident_b[:])
-        sx0 = exp_q(0)
-        sx1 = exp_q(1)
-        ex(0, 0, "V")
-        nc.vector.tensor_copy(out=ftsb[:], in_=pf[:].rearrange("p a o -> p (a o)"))
-        ex(0, 1, "V")
-        pfts = {}
-        pst0 = st_t(0, sx0)
-        st_ev(0, pst0)
-        pfts[(0, 0)] = ft_unit(0, 0)
-        pfts[(1, 0)] = ft_unit(1, 0)
-        if (1, 0) in GUNITS:
-            product(1, 0, pfts[(1, 0)])
-        pst1 = st_t(1, sx1)
-        sx2 = exp_q(2)
-        st_ev(1, pst1)
-        sx3 = exp_q(3)
-        quant_x(0, 0, 2)
-        pfts[(0, 1)] = ft_unit(0, 1)
-        pfts[(1, 1)] = ft_unit(1, 1)
-        tx(0, 2)
-        tx(0, 3)
-        ex(0, 2)
-        ex(0, 3)
-        if EARLY1:
-            stage_a(1)
-        for g, q in ((0, 0), (1, 0), (0, 1), (1, 1)):
-            if (g, q) not in GUNITS:
-                product(g, q, pfts[(g, q)])
-        pst2 = st_t(2, sx2)
-        st_ev(2, pst2)
-        pst3 = st_t(3, sx3)
-        st_ev(3, pst3)
-        for u in GUNITS:
-            if u[1] >= 2:
-                product(u[0], u[1], ft_unit(u[0], u[1]))
-        pb = psum.tile([P, O], BF16, name="pb", tag="tp", bufs=TPB)
+            nc.tensor.transpose(feat_bank_t[:, a, :], feat[:, 2 * a : 2 * a + 2, :].rearrange("p t c -> p (t c)"), ident_b[:])
+        rep0 = exp_repeated(0)
+        rep1 = exp_repeated(1)
+        regroup_x(0, 0, "vector")
+        nc.vector.tensor_copy(out=feat_t[:], in_=feat_bank_t[:].rearrange("p a o -> p (a o)"))
+        regroup_x(0, 1, "vector")
+        feat_banks = {}
+        keep_spat(0, transpose_spat(rep0))
+        feat_banks[(0, 0)] = select_feat(0, 0)
+        feat_banks[(1, 0)] = select_feat(1, 0)
+        spat_bank1 = transpose_spat(rep1)
+        rep2 = exp_repeated(2)
+        keep_spat(1, spat_bank1)
+        rep3 = exp_repeated(3)
+        quantise_x(0, 0, 2)
+        feat_banks[(0, 1)] = select_feat(0, 1)
+        feat_banks[(1, 1)] = select_feat(1, 1)
+        transpose_x(0, 2)
+        transpose_x(0, 3)
+        regroup_x(0, 2, "scalar")
+        regroup_x(0, 3, "scalar")
+        for q in range(2):
+            for g in range(2):
+                build_w(g, q, feat_banks[(g, q)])
+        keep_spat(2, transpose_spat(rep2))
+        keep_spat(3, transpose_spat(rep3))
+        bias_bank = transpose_bank([P, O], BF16, "pb")
         for h in range(2):
-            nc.tensor.matmul(out=pb[:, 512 * h : 512 * h + 512], lhsT=ones_b[:], rhs=brow[:, 512 * h : 512 * h + 512], start=True, stop=True)
-        nc.scalar.copy(out=bias_sb[:], in_=pb[:])
-        for u in ((0, 2), (1, 2)):
-            if u not in GUNITS:
-                pfts[u] = ft_unit(u[0], u[1])
-        if not EARLY1:
-            stage_a(1)
-        quant_w(0, 0)
-        quant_w(1, 0)
-        group(0, 0, 0, HEAD_WHO[0])
-        group(0, 1, 0, HEAD_WHO[1])
-        if HALF:
-            store_half(0, 0, 0)
-        quant_x(0, 2, 2)
-        group(0, 2, 0, HEAD_WHO[2])
-        group(0, 3, 0, HEAD_WHO[3])
-        if HALF:
-            store_half(0, 1, 0)
-        if QX1_FIRST:
-            quant_x(1)
-        for u in ((0, 2), (1, 2)):
-            if u not in GUNITS:
-                product(u[0], u[1], pfts[u])
-        for u in ((0, 3), (1, 3)):
-            if u not in GUNITS:
-                pfts[u] = ft_unit(u[0], u[1])
-        if not QX1_FIRST:
-            stage_a(2)
-            quant_x(1)
-        for r in range(4):
-            group(1, r, 0, HEAD_WHO[4 + r])
-        if QX1_FIRST:
-            stage_a(2)
-        for u in ((0, 3), (1, 3)):
-            if u not in GUNITS:
-                product(u[0], u[1], pfts[u])
-        quant_w(0, 1)
-        quant_w(1, 1)
-        stage_a(3)
-        for ch in range(2):
-            for r in range(4):
-                group(ch, r, 1, HEAD_WHO[8 + 4 * ch + r])
-                if r % 2 == 1:
-                    if HALF:
-                        store_half(ch, r // 2, 1)
-                    else:
-                        store(ch, r - 1, 2)
-            if ch == 0 and HALF:
-                store_half(1, 0, 0)
-                store_half(1, 1, 0)
-            if ch == 0 or LOOKAHEAD == 2:
-                quant_x(2 + ch)
+            half = slice(HALF * h, HALF * h + HALF)
+            nc.tensor.matmul(out=bias_bank[:, half], lhsT=ones_b[:], rhs=bias_row[:, half], start=True, stop=True)
+        nc.scalar.copy(out=bias_all[:], in_=bias_bank[:])
+        feat_banks[(0, 2)] = select_feat(0, 2)
+        feat_banks[(1, 2)] = select_feat(1, 2)
+        stage_chunk(1)
+        quantise_w(0, 0)
+        quantise_w(1, 0)
 
-        for ch in range(2, 8):
-            nxt = STAGE_AT.get(ch)
-            if nxt is not None:
-                stage_a(nxt)
-            who = EO_LAST if ch == 7 else (EO_6 if ch == 6 else EO_STEADY)
-            for r in range(4):
+        multiply(0, 0, 0, "scalar")
+        multiply(0, 1, 0, "scalar")
+        quantise_x(0, 2, 2)
+        multiply(0, 2, 0, "scalar")
+        multiply(0, 3, 0, "scalar")
+        build_w(0, 2, feat_banks[(0, 2)])
+        build_w(1, 2, feat_banks[(1, 2)])
+        feat_banks[(0, 3)] = select_feat(0, 3)
+        feat_banks[(1, 3)] = select_feat(1, 3)
+        stage_chunk(2)
+        quantise_x(1)
+        for r in range(TILES):
+            multiply(1, r, 0, "scalar")
+        build_w(0, 3, feat_banks[(0, 3)])
+        build_w(1, 3, feat_banks[(1, 3)])
+        quantise_w(0, 1)
+        quantise_w(1, 1)
+        quantise_x(2)
+        stage_chunk(3)
+
+        for n in range(2):
+            for r in range(TILES):
+                multiply(n, r, 1, "vector")
+                if r % 2 == 1:
+                    store(n, r - 1, 2)
+            if n == 0:
+                quantise_x(3)
+
+        for n in range(2, CHUNKS):
+            ahead = n + 2
+            if ahead < CHUNKS:
+                stage_chunk(ahead)
+            for r in range(TILES):
                 for h in range(2):
-                    if 2 * r + h == (QPOS6 if ch == 6 else QPOS) and nxt is not None:
-                        quant_x(nxt)
-                    group(ch, r, h, who[2 * r + h])
-                if ch in TILE_CH:
-                    store(ch, r, 1)
+                    if (r, h) == (2, 1) and ahead < CHUNKS:
+                        quantise_x(ahead)
+                    multiply(n, r, h, "scalar" if (r % 2, h) == (0, 0) else "vector")
+                if n == CHUNKS - 1:
+                    store(n, r, 1)
                 elif r % 2 == 1:
-                    store(ch, r - 1, 2)
+                    store(n, r - 1, 2)

@@ -314,7 +314,7 @@ def tile_gaussianspatialxfeaturelinear_t_kernel(tc, x, cx, cy, sigma, features, 
                 for h in range(2):
                     if (r, h) == (2, 1) and ahead < CHUNKS:
                         quantise_x(ahead)
-                    multiply(n, r, h, "scalar" if (r % 2, h) == (0, 0) else "vector")
+                    multiply(n, r, h, "vector")
                 if n == CHUNKS - 1:
                     store(n, r, 1)
                 elif r % 2 == 1:

@@ -15,9 +15,14 @@ P = 128
 B, C, O, K = 4096, 64, 1024, 1024
 HALF = 512
 QUARTER = 256
+SLABS = O // P
 TILES = 4
 CHUNKS = B // (TILES * P)
-TRANSPOSE_BANKS = 3
+MX_ALIGN = 64
+PSUM_BANKS = 8
+RING3 = 3
+X_BF16_BUFS = 3
+Y_PAIR_BUFS = 6
 FLOPS = 2 * B * K * O
 
 
@@ -26,80 +31,83 @@ def tile_gaussianspatialxfeaturelinear_t_kernel(tc, x, cx, cy, sigma, features, 
     with ExitStack() as ctx:
         const = ctx.enter_context(tc.tile_pool(name="const", bufs=1))
         xin = ctx.enter_context(tc.tile_pool(name="xin", bufs=1))
-        stage = ctx.enter_context(tc.tile_pool(name="stage", bufs=3))
-        outp = ctx.enter_context(tc.tile_pool(name="outp", bufs=6))
-        psum = ctx.enter_context(tc.psum_pool(name="psum", bufs=4))
+        rotating = ctx.enter_context(tc.tile_pool(name="rotating", bufs=X_BF16_BUFS))
+        outp = ctx.enter_context(tc.tile_pool(name="outp", bufs=Y_PAIR_BUFS))
+        psum = ctx.enter_context(tc.psum_pool(name="psum", bufs=PSUM_BANKS - RING3))
         ctx.enter_context(tc.manual_schedule())
 
-        x_chunks = x.rearrange("(n p r) c w h -> n p r (c w h)", p=P, r=TILES)
+        x_chunks = x.rearrange("(n p r) c i j -> n p r (c i j)", p=P, r=TILES)
         y_chunks = out.rearrange("(n p r) o -> n p r o", p=P, r=TILES)
 
-        def transpose_bank(shape, dtype, name):
-            return psum.tile(shape, dtype, name=name, tag="tp", bufs=TRANSPOSE_BANKS)
+        def bank_of_three(shape, dtype, name):
+            return psum.tile(shape, dtype, name=name, tag="ring3", bufs=RING3)
 
-        def matmul_bank(shape, dtype, name):
-            return psum.tile(shape, dtype, name=name, tag="acc", bufs=8 - TRANSPOSE_BANKS)
+        def bank_of_five(shape, dtype, name):
+            return psum.tile(shape, dtype, name=name, tag="ring5")
 
-        ident_b = const.tile([P, P], BF16, name="ident_b")
-        ident_f = const.tile([P, P], F32, name="ident_f")
-        make_identity(nc, ident_b[:])
-        make_identity(nc, ident_f[:])
-        vec_rows = const.tile([P, P], BF16, name="zrows")
+        ident_bf16 = const.tile([P, P], BF16, name="ident_bf16")
+        ident_f32 = const.tile([P, P], F32, name="ident_f32")
+        make_identity(nc, ident_bf16[:])
+        make_identity(nc, ident_f32[:])
+        vec_rows = const.tile([P, P], BF16, name="vec_rows")
         nc.vector.memset(vec_rows[:], 0.0)
-        bias_row = const.tile([P, O], BF16, name="brow")
+        bias_row = const.tile([P, O], BF16, name="bias_row")
         nc.vector.memset(bias_row[:], 0.0)
-        ones_b = const.tile([P, P], BF16, name="ones_b")
-        nc.vector.memset(ones_b[:], 1.0)
-        zero_col = const.tile([P, 1], F32, name="warm")
+        ones = const.tile([P, P], BF16, name="ones")
+        nc.vector.memset(ones[:], 1.0)
+        zero_col = const.tile([P, 1], F32, name="zero_col")
         nc.vector.memset(zero_col[:], 0.0)
         grid = const.tile([P, 4], F32, name="grid")
         for i in range(4):
             nc.vector.memset(grid[:, i : i + 1], i - 1.5)
-        select = const.tile([P, 8 * P], BF16, name="sel")
+        select = const.tile([P, 8 * P], BF16, name="select")
         nc.vector.tensor_copy(
-            out=select[:].rearrange("p (r s) -> p r s", s=8),
-            in_=ident_b[:].unsqueeze(2).to_broadcast([P, P, 8]),
+            out=select[:].rearrange("p (row rep) -> p row rep", rep=8),
+            in_=ident_bf16[:].unsqueeze(2).to_broadcast([P, P, 8]),
         )
 
-        for n, vec in enumerate((cx, cy, sigma)):
-            nc.sync.dma_start(out=vec_rows[8 * n : 8 * n + 8, :], in_=vec.rearrange("(t p) a b c -> t (p a b c)", p=P))
-        nc.scalar.dma_start(out=bias_row[0:1, :], in_=bias.rearrange("(a o) -> a o", a=1))
-        feat = const.tile([P, 8, C], BF16, name="fsb")
+        for v, vec in enumerate((cx, cy, sigma)):
+            nc.sync.dma_start(
+                out=vec_rows[SLABS * v : SLABS * v + SLABS, :],
+                in_=vec.rearrange("(slab p) x1 x2 x3 -> slab (p x1 x2 x3)", p=P),
+            )
+        nc.scalar.dma_start(out=bias_row[0:1, :], in_=bias.rearrange("(row o) -> row o", row=1))
+        feat = const.tile([P, SLABS, C], BF16, name="feat")
         x_raw = []
         for n in range(CHUNKS):
-            x_tile = xin.tile([P, TILES, K], BF16, name="x%d" % n)
-            x_raw.append(x_tile)
+            raw = xin.tile([P, TILES, K], BF16, name="x_raw%d" % n)
+            x_raw.append(raw)
             if n == 0:
-                nc.sync.dma_start(out=x_tile[:, 0:2, :], in_=x_chunks[n][:, 0:2, :])
-                nc.sync.dma_start(out=feat[:], in_=features.rearrange("(t p) c a b -> p t (c a b)", p=P))
-                nc.sync.dma_start(out=x_tile[:, 2:4, :], in_=x_chunks[n][:, 2:4, :])
+                nc.sync.dma_start(out=raw[:, 0:2, :], in_=x_chunks[n][:, 0:2, :])
+                nc.sync.dma_start(out=feat[:], in_=features.rearrange("(slab p) c x1 x2 -> p slab (c x1 x2)", p=P))
+                nc.sync.dma_start(out=raw[:, 2:4, :], in_=x_chunks[n][:, 2:4, :])
             else:
-                nc.sync.dma_start(out=x_tile[:], in_=x_chunks[n])
-        one_col = const.tile([P, 1], F32, name="warm2")
+                nc.sync.dma_start(out=raw[:], in_=x_chunks[n])
+        one_col = const.tile([P, 1], F32, name="one_col")
         nc.scalar.activation(out=one_col[:], in_=zero_col[:], func=ACT.Exp)
 
-        w_bf16 = const.tile([P, 2, O, 4], BF16, name="gw", align_bytes=64)
-        w_words = const.tile([P, 2, O], U32, name="wcod", align_bytes=64)
-        w_scales = const.tile([P, 2, O], U8, name="wscl", align_bytes=64)
-        x_words = [const.tile([P, TILES * 2 * P], U32, name="xcod%d" % n, align_bytes=64) for n in range(CHUNKS)]
-        x_scales = [const.tile([P, TILES * 2 * P], U8, name="xscl%d" % n, align_bytes=64) for n in range(CHUNKS)]
-        bias_all = const.tile([P, O], BF16, name="bias_sb")
-        spat_t = const.tile([P, 4, 2, QUARTER], F32, name="stsb")
-        feat_t = const.tile([P, 4 * P], BF16, name="ftsb")
+        w_bf16 = const.tile([P, 2, O, 4], BF16, name="w_bf16", align_bytes=MX_ALIGN)
+        w_words = const.tile([P, 2, O], U32, name="w_words", align_bytes=MX_ALIGN)
+        w_scales = const.tile([P, 2, O], U8, name="w_scales", align_bytes=MX_ALIGN)
+        x_words = [const.tile([P, TILES * 2 * P], U32, name="x_words%d" % n, align_bytes=MX_ALIGN) for n in range(CHUNKS)]
+        x_scales = [const.tile([P, TILES * 2 * P], U8, name="x_scales%d" % n, align_bytes=MX_ALIGN) for n in range(CHUNKS)]
+        bias_all = const.tile([P, O], BF16, name="bias_all")
+        spat_t = const.tile([P, 4, 2, QUARTER], F32, name="spat_t")
+        feat_t = const.tile([P, 4 * P], BF16, name="feat_t")
         x_bf16 = {}
         x_banks = {}
         y_pairs = {}
 
         def transpose_x(n, r):
-            bank = transpose_bank([P, 4, P], F32, "tp")
+            bank = bank_of_three([P, 4, P], F32, "x_bank")
             words = x_raw[n][:, r, :].bitcast(F32)
-            for s in range(4):
-                nc.tensor.transpose(bank[:, s, :], words[:, P * s : P * s + P], ident_f[:])
+            for gu in range(4):
+                nc.tensor.transpose(bank[:, gu, :], words[:, P * gu : P * gu + P], ident_f32[:])
             x_banks[(n, r)] = bank
 
         def regroup_x(n, r, engine):
             if n not in x_bf16:
-                x_bf16[n] = stage.tile([P, TILES, K], BF16, name="gx", align_bytes=64)
+                x_bf16[n] = rotating.tile([P, TILES, K], BF16, name="x_bf16", align_bytes=MX_ALIGN)
             dst = x_bf16[n][:, r, :].bitcast(F32).rearrange("p (g b u) -> p g b u", g=2, u=2)
             src = x_banks[(n, r)][:].rearrange("p (g u) b -> p g b u", g=2)
             if engine == "scalar":
@@ -123,9 +131,9 @@ def tile_gaussianspatialxfeaturelinear_t_kernel(tc, x, cx, cy, sigma, features, 
 
         def multiply(n, r, h, way_out):
             if (n, r // 2) not in y_pairs:
-                y_pairs[(n, r // 2)] = outp.tile([P, 2, O], F32, name="osb")
+                y_pairs[(n, r // 2)] = outp.tile([P, 2, O], F32, name="y_pair")
             half = slice(HALF * h, HALF * h + HALF)
-            bank = matmul_bank([P, HALF], F32, "acc")
+            bank = bank_of_five([P, HALF], F32, "y_bank")
             for g in range(2):
                 cols = slice(2 * P * r + P * g, 2 * P * r + P * g + P)
                 nc.tensor.matmul_mx(
@@ -150,69 +158,73 @@ def tile_gaussianspatialxfeaturelinear_t_kernel(tc, x, cx, cy, sigma, features, 
                 in_=y_pairs[(n, first // 2)][:, first % 2 : first % 2 + count, :],
             )
 
-        vec_bank = matmul_bank([P, P], BF16, "pz")
-        nc.tensor.transpose(vec_bank[:], vec_rows[:], ident_b[:])
-        vec_cols = const.tile([P, 24], F32, name="zt")
-        nc.vector.tensor_copy(out=vec_cols[:], in_=vec_bank[:, 0:24])
-        dist = const.tile([P, 2, 8, 4], F32, name="dxy")
+        vec_bank = bank_of_five([P, P], BF16, "vec_bank")
+        nc.tensor.transpose(vec_bank[:], vec_rows[:], ident_bf16[:])
+        vec_cols = const.tile([P, 3 * SLABS], F32, name="vec_cols")
+        nc.vector.tensor_copy(out=vec_cols[:], in_=vec_bank[:, 0 : 3 * SLABS])
+        dist = const.tile([P, 2, SLABS, 4], F32, name="dist")
         nc.vector.tensor_tensor(
             out=dist[:],
-            in0=vec_cols[:, 0:16].rearrange("p (a t) -> p a t", a=2).unsqueeze(3).to_broadcast([P, 2, 8, 4]),
-            in1=grid[:].unsqueeze(1).unsqueeze(1).to_broadcast([P, 2, 8, 4]),
+            in0=vec_cols[:, 0 : 2 * SLABS]
+            .rearrange("p (axis slab) -> p axis slab", axis=2)
+            .unsqueeze(3)
+            .to_broadcast([P, 2, SLABS, 4]),
+            in1=grid[:].unsqueeze(1).unsqueeze(1).to_broadcast([P, 2, SLABS, 4]),
             op=ALU.subtract,
         )
-        dist_sq = const.tile([P, 2, 8, 4], F32, name="sq")
+        dist_sq = const.tile([P, 2, SLABS, 4], F32, name="dist_sq")
         nc.vector.tensor_tensor(out=dist_sq[:], in0=dist[:], in1=dist[:], op=ALU.mult)
-        sigma_sq = const.tile([P, 8], F32, name="s2")
-        nc.vector.tensor_tensor(out=sigma_sq[:], in0=vec_cols[:, 16:24], in1=vec_cols[:, 16:24], op=ALU.mult)
-        inv_sigma_sq = const.tile([P, 8], F32, name="rinv")
+        sigma_cols = vec_cols[:, 2 * SLABS : 3 * SLABS]
+        sigma_sq = const.tile([P, SLABS], F32, name="sigma_sq")
+        nc.vector.tensor_tensor(out=sigma_sq[:], in0=sigma_cols, in1=sigma_cols, op=ALU.mult)
+        inv_sigma_sq = const.tile([P, SLABS], F32, name="inv_sigma_sq")
         nc.vector.reciprocal(out=inv_sigma_sq[:], in_=sigma_sq[:])
-        dist_sum = const.tile([P, 8, 2, 4, 2], F32, name="dd")
+        dist_sum = const.tile([P, SLABS, 2, 4, 2], F32, name="dist_sum")
         for e in range(2):
             nc.vector.tensor_tensor(
                 out=dist_sum[:, :, e, :, :],
-                in0=dist_sq[:, 0, :, :].unsqueeze(3).to_broadcast([P, 8, 4, 2]),
-                in1=dist_sq[:, 1, :, e::2].unsqueeze(2).to_broadcast([P, 8, 4, 2]),
+                in0=dist_sq[:, 0, :, :].unsqueeze(3).to_broadcast([P, SLABS, 4, 2]),
+                in1=dist_sq[:, 1, :, e::2].unsqueeze(2).to_broadcast([P, SLABS, 4, 2]),
                 op=ALU.add,
             )
-        exponent = const.tile([P, 8, 16], F32, name="qq")
+        exponent = const.tile([P, SLABS, 16], F32, name="exponent")
         nc.vector.tensor_tensor(
             out=exponent[:],
-            in0=dist_sum[:].rearrange("p t e i j -> p t (e i j)"),
-            in1=inv_sigma_sq[:].unsqueeze(2).to_broadcast([P, 8, 16]),
+            in0=dist_sum[:].rearrange("p slab e i j2 -> p slab (e i j2)"),
+            in1=inv_sigma_sq[:].unsqueeze(2).to_broadcast([P, SLABS, 16]),
             op=ALU.mult,
         )
 
         def exp_repeated(q):
-            rep = stage.tile([P, 4, P], F32, name="sx", bufs=2)
+            repeated = rotating.tile([P, 4, P], F32, name="repeated", bufs=2)
             nc.scalar.activation(
-                out=rep[:].rearrange("p b (s m) -> p b s m", m=8),
+                out=repeated[:].rearrange("p blk (rep pt) -> p blk rep pt", pt=8),
                 in_=exponent[:, 2 * q : 2 * q + 2, :]
-                .rearrange("p t (e m) -> p (t e) m", e=2)
+                .rearrange("p slab (e pt) -> p (slab e) pt", e=2)
                 .unsqueeze(2)
                 .to_broadcast([P, 4, 16, 8]),
                 func=ACT.Exp,
                 scale=-1.0,
             )
-            return rep
+            return repeated
 
-        def transpose_spat(rep):
-            bank = transpose_bank([P, 4, P], F32, "pst")
+        def transpose_spat(repeated):
+            bank = bank_of_three([P, 4, P], F32, "spat_bank")
             for e in range(2):
-                for t in range(2):
-                    nc.tensor.transpose(bank[:, 2 * e + t, :], rep[:, 2 * t + e, :], ident_f[:])
+                for odd in range(2):
+                    nc.tensor.transpose(bank[:, 2 * e + odd, :], repeated[:, 2 * odd + e, :], ident_f32[:])
             return bank
 
         def keep_spat(q, bank):
-            nc.scalar.copy(out=spat_t[:, q, :, :], in_=bank[:].rearrange("p (e t) o -> p e (t o)", e=2))
+            nc.scalar.copy(out=spat_t[:, q, :, :], in_=bank[:].rearrange("p (e odd) s -> p e (odd s)", e=2))
 
         def select_feat(g, q):
-            bank = matmul_bank([P, 2, QUARTER], F32, "pft")
+            bank = bank_of_five([P, 2, QUARTER], F32, "feat_bank")
             for u in range(2):
-                for s in range(2):
-                    m = 4 * s + 2 * g + u
+                for odd in range(2):
+                    m = 4 * odd + 2 * g + u
                     nc.tensor.matmul(
-                        out=bank[:, u, P * s : P * s + P],
+                        out=bank[:, u, P * odd : P * odd + P],
                         lhsT=select[:, P * m : P * m + P],
                         rhs=feat_t[:, P * q : P * q + P],
                         start=True,
@@ -234,27 +246,29 @@ def tile_gaussianspatialxfeaturelinear_t_kernel(tc, x, cx, cy, sigma, features, 
             nc.vector.quantize_mx(
                 out=w_words[:, g, half].bitcast(FP8X4),
                 scales=w_scales[:, g, half],
-                in_=w_bf16[:, g, half, :].rearrange("p o t -> p (o t)"),
+                in_=w_bf16[:, g, half, :].rearrange("p o ue -> p (o ue)"),
             )
 
         transpose_x(0, 0)
         transpose_x(0, 1)
-        feat_bank_t = matmul_bank([P, 4, P], BF16, "pf")
-        for a in range(4):
-            nc.tensor.transpose(feat_bank_t[:, a, :], feat[:, 2 * a : 2 * a + 2, :].rearrange("p t c -> p (t c)"), ident_b[:])
-        rep0 = exp_repeated(0)
-        rep1 = exp_repeated(1)
+        feat_t_bank = bank_of_five([P, 4, P], BF16, "feat_t_bank")
+        for q in range(4):
+            nc.tensor.transpose(
+                feat_t_bank[:, q, :], feat[:, 2 * q : 2 * q + 2, :].rearrange("p odd c -> p (odd c)"), ident_bf16[:]
+            )
+        repeated0 = exp_repeated(0)
+        repeated1 = exp_repeated(1)
         regroup_x(0, 0, "vector")
-        nc.vector.tensor_copy(out=feat_t[:], in_=feat_bank_t[:].rearrange("p a o -> p (a o)"))
+        nc.vector.tensor_copy(out=feat_t[:], in_=feat_t_bank[:].rearrange("p q s -> p (q s)"))
         regroup_x(0, 1, "vector")
         feat_banks = {}
-        keep_spat(0, transpose_spat(rep0))
+        keep_spat(0, transpose_spat(repeated0))
         feat_banks[(0, 0)] = select_feat(0, 0)
         feat_banks[(1, 0)] = select_feat(1, 0)
-        spat_bank1 = transpose_spat(rep1)
-        rep2 = exp_repeated(2)
+        spat_bank1 = transpose_spat(repeated1)
+        repeated2 = exp_repeated(2)
         keep_spat(1, spat_bank1)
-        rep3 = exp_repeated(3)
+        repeated3 = exp_repeated(3)
         quantise_x(0, 0, 2)
         feat_banks[(0, 1)] = select_feat(0, 1)
         feat_banks[(1, 1)] = select_feat(1, 1)
@@ -265,12 +279,12 @@ def tile_gaussianspatialxfeaturelinear_t_kernel(tc, x, cx, cy, sigma, features, 
         for q in range(2):
             for g in range(2):
                 build_w(g, q, feat_banks[(g, q)])
-        keep_spat(2, transpose_spat(rep2))
-        keep_spat(3, transpose_spat(rep3))
-        bias_bank = transpose_bank([P, O], BF16, "pb")
+        keep_spat(2, transpose_spat(repeated2))
+        keep_spat(3, transpose_spat(repeated3))
+        bias_bank = bank_of_three([P, O], BF16, "bias_bank")
         for h in range(2):
             half = slice(HALF * h, HALF * h + HALF)
-            nc.tensor.matmul(out=bias_bank[:, half], lhsT=ones_b[:], rhs=bias_row[:, half], start=True, stop=True)
+            nc.tensor.matmul(out=bias_bank[:, half], lhsT=ones[:], rhs=bias_row[:, half], start=True, stop=True)
         nc.scalar.copy(out=bias_all[:], in_=bias_bank[:])
         feat_banks[(0, 2)] = select_feat(0, 2)
         feat_banks[(1, 2)] = select_feat(1, 2)
@@ -314,7 +328,7 @@ def tile_gaussianspatialxfeaturelinear_t_kernel(tc, x, cx, cy, sigma, features, 
                 for h in range(2):
                     if (r, h) == (2, 1) and ahead < CHUNKS:
                         quantise_x(ahead)
-                    multiply(n, r, h, "vector")
+                    multiply(n, r, h, "scalar" if (r % 2, h) == (0, 0) else "vector")
                 if n == CHUNKS - 1:
                     store(n, r, 1)
                 elif r % 2 == 1:

from contextlib import ExitStack

import concourse.mybir as mybir
from concourse.masks import make_identity

F32 = mybir.dt.float32
BF16 = mybir.dt.bfloat16
U32 = mybir.dt.uint32
U8 = mybir.dt.uint8
FP8X4 = mybir.dt.float8_e4m3fn_x4
ALU = mybir.AluOpType
ACT = mybir.ActivationFunctionType

P = 128
B, C, O, K = 4096, 64, 1024, 1024
HALF = 512
QUARTER = 256
SLABS = O // P
TILES = 4
CHUNKS = B // (TILES * P)
MX_ALIGN = 64
PSUM_BANKS = 8
RING3 = 3
X_BF16_BUFS = 3
Y_PAIR_BUFS = 6
FLOPS = 2 * B * K * O


def tile_gaussianspatialxfeaturelinear_t_kernel(tc, x, cx, cy, sigma, features, bias, out):
    nc = tc.nc
    with ExitStack() as ctx:
        const = ctx.enter_context(tc.tile_pool(name="const", bufs=1))
        xin = ctx.enter_context(tc.tile_pool(name="xin", bufs=1))
        rotating = ctx.enter_context(tc.tile_pool(name="rotating", bufs=X_BF16_BUFS))
        outp = ctx.enter_context(tc.tile_pool(name="outp", bufs=Y_PAIR_BUFS))
        psum = ctx.enter_context(tc.psum_pool(name="psum", bufs=PSUM_BANKS - RING3))
        ctx.enter_context(tc.manual_schedule())

        x_chunks = x.rearrange("(n p r) c i j -> n p r (c i j)", p=P, r=TILES)
        y_chunks = out.rearrange("(n p r) o -> n p r o", p=P, r=TILES)

        def bank_of_three(shape, dtype, name):
            return psum.tile(shape, dtype, name=name, tag="ring3", bufs=RING3)

        def bank_of_five(shape, dtype, name):
            return psum.tile(shape, dtype, name=name, tag="ring5")

        ident_bf16 = const.tile([P, P], BF16, name="ident_bf16")
        ident_f32 = const.tile([P, P], F32, name="ident_f32")
        make_identity(nc, ident_bf16[:])
        make_identity(nc, ident_f32[:])
        vec_rows = const.tile([P, P], BF16, name="vec_rows")
        nc.vector.memset(vec_rows[:], 0.0)
        bias_row = const.tile([P, O], BF16, name="bias_row")
        nc.vector.memset(bias_row[:], 0.0)
        ones = const.tile([P, P], BF16, name="ones")
        nc.vector.memset(ones[:], 1.0)
        zero_col = const.tile([P, 1], F32, name="zero_col")
        nc.vector.memset(zero_col[:], 0.0)
        grid = const.tile([P, 4], F32, name="grid")
        for i in range(4):
            nc.vector.memset(grid[:, i : i + 1], i - 1.5)
        select = const.tile([P, 8 * P], BF16, name="select")
        nc.vector.tensor_copy(
            out=select[:].rearrange("p (row rep) -> p row rep", rep=8),
            in_=ident_bf16[:].unsqueeze(2).to_broadcast([P, P, 8]),
        )

        for v, vec in enumerate((cx, cy, sigma)):
            nc.sync.dma_start(
                out=vec_rows[SLABS * v : SLABS * v + SLABS, :],
                in_=vec.rearrange("(slab p) x1 x2 x3 -> slab (p x1 x2 x3)", p=P),
            )
        nc.scalar.dma_start(out=bias_row[0:1, :], in_=bias.rearrange("(row o) -> row o", row=1))
        feat = const.tile([P, SLABS, C], BF16, name="feat")
        x_raw = []
        for n in range(CHUNKS):
            raw = xin.tile([P, TILES, K], BF16, name="x_raw%d" % n)
            x_raw.append(raw)
            if n == 0:
                nc.sync.dma_start(out=raw[:, 0:2, :], in_=x_chunks[n][:, 0:2, :])
                nc.sync.dma_start(out=feat[:], in_=features.rearrange("(slab p) c x1 x2 -> p slab (c x1 x2)", p=P))
                nc.sync.dma_start(out=raw[:, 2:4, :], in_=x_chunks[n][:, 2:4, :])
            else:
                nc.sync.dma_start(out=raw[:], in_=x_chunks[n])
        one_col = const.tile([P, 1], F32, name="one_col")
        nc.scalar.activation(out=one_col[:], in_=zero_col[:], func=ACT.Exp)

        w_bf16 = const.tile([P, 2, O, 4], BF16, name="w_bf16", align_bytes=MX_ALIGN)
        w_words = const.tile([P, 2, O], U32, name="w_words", align_bytes=MX_ALIGN)
        w_scales = const.tile([P, 2, O], U8, name="w_scales", align_bytes=MX_ALIGN)
        x_words = [const.tile([P, TILES * 2 * P], U32, name="x_words%d" % n, align_bytes=MX_ALIGN) for n in range(CHUNKS)]
        x_scales = [const.tile([P, TILES * 2 * P], U8, name="x_scales%d" % n, align_bytes=MX_ALIGN) for n in range(CHUNKS)]
        bias_all = const.tile([P, O], BF16, name="bias_all")
        spat_t = const.tile([P, 4, 2, QUARTER], F32, name="spat_t")
        feat_t = const.tile([P, 4 * P], BF16, name="feat_t")
        x_bf16 = {}
        x_banks = {}
        y_pairs = {}

        def transpose_x(n, r):
            bank = bank_of_three([P, 4, P], F32, "x_bank")
            words = x_raw[n][:, r, :].bitcast(F32)
            for gu in range(4):
                nc.tensor.transpose(bank[:, gu, :], words[:, P * gu : P * gu + P], ident_f32[:])
            x_banks[(n, r)] = bank

        def regroup_x(n, r, engine):
            if n not in x_bf16:
                x_bf16[n] = rotating.tile([P, TILES, K], BF16, name="x_bf16", align_bytes=MX_ALIGN)
            dst = x_bf16[n][:, r, :].bitcast(F32).rearrange("p (g b u) -> p g b u", g=2, u=2)
            src = x_banks[(n, r)][:].rearrange("p (g u) b -> p g b u", g=2)
            if engine == "scalar":
                nc.scalar.copy(out=dst, in_=src)
            else:
                nc.vector.tensor_copy(out=dst, in_=src)

        def stage_chunk(n):
            for r in range(TILES):
                transpose_x(n, r)
            for r in range(TILES):
                regroup_x(n, r, "scalar")

        def quantise_x(n, first=0, count=TILES):
            cols = slice(2 * P * first, 2 * P * (first + count))
            nc.vector.quantize_mx(
                out=x_words[n][:, cols].bitcast(FP8X4),
                scales=x_scales[n][:, cols],
                in_=x_bf16[n][:, first : first + count, :].rearrange("p r k -> p (r k)"),
            )

        def multiply(n, r, h, way_out):
            if (n, r // 2) not in y_pairs:
                y_pairs[(n, r // 2)] = outp.tile([P, 2, O], F32, name="y_pair")
            half = slice(HALF * h, HALF * h + HALF)
            bank = bank_of_five([P, HALF], F32, "y_bank")
            for g in range(2):
                cols = slice(2 * P * r + P * g, 2 * P * r + P * g + P)
                nc.tensor.matmul_mx(
                    out=bank[:],
                    lhsT=x_words[n][:, cols].bitcast(FP8X4),
                    lhsT_scale=x_scales[n][:, cols],
                    rhs=w_words[:, g, half].bitcast(FP8X4),
                    rhs_scale=w_scales[:, g, half],
                    start=(g == 0),
                    stop=(g == 1),
                )
            dst = y_pairs[(n, r // 2)][:, r % 2, half]
            if way_out == "vector":
                nc.vector.tensor_tensor(out=dst, in0=bank[:], in1=bias_all[:, half], op=ALU.add)
            else:
                nc.scalar.copy(out=dst, in_=bank[:])
                nc.gpsimd.tensor_tensor(out=dst, in0=dst, in1=bias_all[:, half], op=ALU.add)

        def store(n, first, count):
            nc.sync.dma_start(
                out=y_chunks[n][:, first : first + count, :],
                in_=y_pairs[(n, first // 2)][:, first % 2 : first % 2 + count, :],
            )

        vec_bank = bank_of_five([P, P], BF16, "vec_bank")
        nc.tensor.transpose(vec_bank[:], vec_rows[:], ident_bf16[:])
        vec_cols = const.tile([P, 3 * SLABS], F32, name="vec_cols")
        nc.vector.tensor_copy(out=vec_cols[:], in_=vec_bank[:, 0 : 3 * SLABS])
        dist = const.tile([P, 2, SLABS, 4], F32, name="dist")
        nc.vector.tensor_tensor(
            out=dist[:],
            in0=vec_cols[:, 0 : 2 * SLABS]
            .rearrange("p (axis slab) -> p axis slab", axis=2)
            .unsqueeze(3)
            .to_broadcast([P, 2, SLABS, 4]),
            in1=grid[:].unsqueeze(1).unsqueeze(1).to_broadcast([P, 2, SLABS, 4]),
            op=ALU.subtract,
        )
        dist_sq = const.tile([P, 2, SLABS, 4], F32, name="dist_sq")
        nc.vector.tensor_tensor(out=dist_sq[:], in0=dist[:], in1=dist[:], op=ALU.mult)
        sigma_cols = vec_cols[:, 2 * SLABS : 3 * SLABS]
        sigma_sq = const.tile([P, SLABS], F32, name="sigma_sq")
        nc.vector.tensor_tensor(out=sigma_sq[:], in0=sigma_cols, in1=sigma_cols, op=ALU.mult)
        inv_sigma_sq = const.tile([P, SLABS], F32, name="inv_sigma_sq")
        nc.vector.reciprocal(out=inv_sigma_sq[:], in_=sigma_sq[:])
        dist_sum = const.tile([P, SLABS, 2, 4, 2], F32, name="dist_sum")
        for e in range(2):
            nc.vector.tensor_tensor(
                out=dist_sum[:, :, e, :, :],
                in0=dist_sq[:, 0, :, :].unsqueeze(3).to_broadcast([P, SLABS, 4, 2]),
                in1=dist_sq[:, 1, :, e::2].unsqueeze(2).to_broadcast([P, SLABS, 4, 2]),
                op=ALU.add,
            )
        exponent = const.tile([P, SLABS, 16], F32, name="exponent")
        nc.vector.tensor_tensor(
            out=exponent[:],
            in0=dist_sum[:].rearrange("p slab e i j2 -> p slab (e i j2)"),
            in1=inv_sigma_sq[:].unsqueeze(2).to_broadcast([P, SLABS, 16]),
            op=ALU.mult,
        )

        def exp_repeated(q):
            repeated = rotating.tile([P, 4, P], F32, name="repeated", bufs=2)
            nc.scalar.activation(
                out=repeated[:].rearrange("p blk (rep pt) -> p blk rep pt", pt=8),
                in_=exponent[:, 2 * q : 2 * q + 2, :]
                .rearrange("p slab (e pt) -> p (slab e) pt", e=2)
                .unsqueeze(2)
                .to_broadcast([P, 4, 16, 8]),
                func=ACT.Exp,
                scale=-1.0,
            )
            return repeated

        def transpose_spat(repeated):
            bank = bank_of_three([P, 4, P], F32, "spat_bank")
            for e in range(2):
                for odd in range(2):
                    nc.tensor.transpose(bank[:, 2 * e + odd, :], repeated[:, 2 * odd + e, :], ident_f32[:])
            return bank

        def keep_spat(q, bank):
            nc.scalar.copy(out=spat_t[:, q, :, :], in_=bank[:].rearrange("p (e odd) s -> p e (odd s)", e=2))

        def select_feat(g, q):
            bank = bank_of_five([P, 2, QUARTER], F32, "feat_bank")
            for u in range(2):
                for odd in range(2):
                    m = 4 * odd + 2 * g + u
                    nc.tensor.matmul(
                        out=bank[:, u, P * odd : P * odd + P],
                        lhsT=select[:, P * m : P * m + P],
                        rhs=feat_t[:, P * q : P * q + P],
                        start=True,
                        stop=True,
                    )
            return bank

        def build_w(g, q, feat_bank):
            shape = [P, QUARTER, 2, 2]
            nc.vector.tensor_tensor(
                out=w_bf16[:, g, QUARTER * q : QUARTER * q + QUARTER, :].rearrange("p o (u e) -> p o u e", u=2),
                in0=feat_bank[:].rearrange("p u o -> p o u").unsqueeze(3).to_broadcast(shape),
                in1=spat_t[:, q, :, :].rearrange("p e o -> p o e").unsqueeze(2).to_broadcast(shape),
                op=ALU.mult,
            )

        def quantise_w(g, h):
            half = slice(HALF * h, HALF * h + HALF)
            nc.vector.quantize_mx(
                out=w_words[:, g, half].bitcast(FP8X4),
                scales=w_scales[:, g, half],
                in_=w_bf16[:, g, half, :].rearrange("p o ue -> p (o ue)"),
            )

        transpose_x(0, 0)
        transpose_x(0, 1)
        feat_t_bank = bank_of_five([P, 4, P], BF16, "feat_t_bank")
        for q in range(4):
            nc.tensor.transpose(
                feat_t_bank[:, q, :], feat[:, 2 * q : 2 * q + 2, :].rearrange("p odd c -> p (odd c)"), ident_bf16[:]
            )
        repeated0 = exp_repeated(0)
        repeated1 = exp_repeated(1)
        regroup_x(0, 0, "vector")
        nc.vector.tensor_copy(out=feat_t[:], in_=feat_t_bank[:].rearrange("p q s -> p (q s)"))
        regroup_x(0, 1, "vector")
        feat_banks = {}
        keep_spat(0, transpose_spat(repeated0))
        feat_banks[(0, 0)] = select_feat(0, 0)
        feat_banks[(1, 0)] = select_feat(1, 0)
        spat_bank1 = transpose_spat(repeated1)
        repeated2 = exp_repeated(2)
        keep_spat(1, spat_bank1)
        repeated3 = exp_repeated(3)
        quantise_x(0, 0, 2)
        feat_banks[(0, 1)] = select_feat(0, 1)
        feat_banks[(1, 1)] = select_feat(1, 1)
        transpose_x(0, 2)
        transpose_x(0, 3)
        regroup_x(0, 2, "scalar")
        regroup_x(0, 3, "scalar")
        for q in range(2):
            for g in range(2):
                build_w(g, q, feat_banks[(g, q)])
        keep_spat(2, transpose_spat(repeated2))
        keep_spat(3, transpose_spat(repeated3))
        bias_bank = bank_of_three([P, O], BF16, "bias_bank")
        for h in range(2):
            half = slice(HALF * h, HALF * h + HALF)
            nc.tensor.matmul(out=bias_bank[:, half], lhsT=ones[:], rhs=bias_row[:, half], start=True, stop=True)
        nc.scalar.copy(out=bias_all[:], in_=bias_bank[:])
        feat_banks[(0, 2)] = select_feat(0, 2)
        feat_banks[(1, 2)] = select_feat(1, 2)
        stage_chunk(1)
        quantise_w(0, 0)
        quantise_w(1, 0)

        multiply(0, 0, 0, "scalar")
        multiply(0, 1, 0, "scalar")
        quantise_x(0, 2, 2)
        multiply(0, 2, 0, "scalar")
        multiply(0, 3, 0, "scalar")
        build_w(0, 2, feat_banks[(0, 2)])
        build_w(1, 2, feat_banks[(1, 2)])
        feat_banks[(0, 3)] = select_feat(0, 3)
        feat_banks[(1, 3)] = select_feat(1, 3)
        stage_chunk(2)
        quantise_x(1)
        for r in range(TILES):
            multiply(1, r, 0, "scalar")
        build_w(0, 3, feat_banks[(0, 3)])
        build_w(1, 3, feat_banks[(1, 3)])
        quantise_w(0, 1)
        quantise_w(1, 1)
        quantise_x(2)
        stage_chunk(3)

        for n in range(2):
            for r in range(TILES):
                multiply(n, r, 1, "vector")
                if r % 2 == 1:
                    store(n, r - 1, 2)
            if n == 0:
                quantise_x(3)

        for n in range(2, CHUNKS):
            ahead = n + 2
            if ahead < CHUNKS:
                stage_chunk(ahead)
            for r in range(TILES):
                for h in range(2):
                    if (r, h) == (2, 1) and ahead < CHUNKS:
                        quantise_x(ahead)
                    multiply(n, r, h, "scalar" if (r % 2, h) == (0, 0) else "vector")
                if n == CHUNKS - 1:
                    store(n, r, 1)
                elif r % 2 == 1:
                    store(n, r - 1, 2)
